import numpy as np
import ml_dtypes


def mxq(x, axis, fmt="e4m3"):
    dtype, down = {"e4m3": (ml_dtypes.float8_e4m3fn, 7), "e5m2": (ml_dtypes.float8_e5m2, 14)}[fmt]
    v = np.moveaxis(np.asarray(x, np.float32).astype(ml_dtypes.bfloat16).astype(np.float64), axis, -1)
    blocks = v.reshape(v.shape[:-1] + (-1, 32))
    amax = np.abs(blocks).max(-1, keepdims=True)
    byte = np.maximum(np.where(amax > 0, np.frexp(amax)[1] - 1 + 127, 0) - down, 1)
    scale = np.exp2(byte - 127.0)
    codes = (blocks / scale).astype(np.float32).astype(dtype).astype(np.float64)
    return np.moveaxis((codes * scale).reshape(v.shape), -1, axis)


WIDE = False


def mx_kscale(k):
    if not WIDE:
        return np.ones(k)
    levels = np.array([10, -10, 5, -5, 0])
    a = np.random.permutation(np.resize(levels, k // 512 * 4)).reshape(k // 512, 4)
    idx = np.arange(k)
    return np.exp2(a[idx // 512, idx % 128 // 32])


BF16 = ml_dtypes.bfloat16


def bf(x):
    return np.asarray(x, np.float32).astype(BF16)


def f64(x):
    return np.asarray(x).astype(np.float64)


E2M1 = np.array([0.0, 0.5, 1.0, 1.5, 2.0, 3.0, 4.0, 6.0, -0.0, -0.5, -1.0, -1.5, -2.0, -3.0, -4.0, -6.0])


def pack_weight(w, fmt):
    k, n = w.shape
    w = f64(bf(w)).reshape(k // 32, 32, n)
    amax = np.abs(w).max(1)
    if fmt == "e4m3":
        byte = np.frexp(amax)[1] - 1 + 127 - 7
    else:
        mant, ex = np.frexp(amax / 6.0)
        byte = np.where(mant > 0.5, ex, ex - 1) + 127
    byte = np.clip(np.where(amax > 0, byte, 1), 1, 254)
    scaled = (w * np.exp2(127.0 - byte)[:, None, :]).reshape(k, n).astype(np.float32)
    by_word = np.ascontiguousarray(scaled.reshape(k // 512, 128, 4, n).transpose(0, 1, 3, 2))
    if fmt == "e4m3":
        words = by_word.astype(ml_dtypes.float8_e4m3fn).view(np.uint8)
    else:
        c = by_word.astype(ml_dtypes.float4_e2m1fn).view(np.uint8) & 0xF
        words = c[..., 0::2] | (c[..., 1::2] << 4)
    return np.ascontiguousarray(words), np.ascontiguousarray(byte.astype(np.uint8).reshape(k // 512, 16, n))


def unpack_weight(words, scales, fmt):
    g, p, n, _ = words.shape
    if fmt == "e4m3":
        vals = np.ascontiguousarray(words).view(ml_dtypes.float8_e4m3fn).astype(np.float64)
    else:
        nib = np.empty((g, p, n, 4), np.uint8)
        nib[..., 0::2] = words & 0xF
        nib[..., 1::2] = words >> 4
        vals = E2M1[nib]
    vals = vals * np.repeat(np.exp2(scales.astype(np.float64) - 127.0), 8, axis=1)[..., None]
    return vals.transpose(0, 1, 3, 2).reshape(g * 512, n)


B, C, H, W, R, G, K = 1, 1024, 8, 16, 8192, 128, 5
PAD = K // 2
KK = K * K
FMT = "e4m3"


def setup_inputs():
    t = mx_kscale(R)
    x = bf(np.random.standard_normal((B, C, H, W)))
    w_reduce = np.random.standard_normal((R, C)) * 1.0 / np.sqrt(C) * t[:, None]
    b_reduce = bf(np.random.standard_normal(R) * 0.5 * t)
    w_span = np.random.standard_normal((KK * G, R)) * 1.5 / np.sqrt(R) / t[None, :]
    b_span = bf(np.random.standard_normal(KK * G) * 0.5)
    w_reduce_words, w_reduce_scales = pack_weight(np.ascontiguousarray(w_reduce.T), FMT)
    w_span_words, w_span_scales = pack_weight(np.ascontiguousarray(w_span.T), FMT)
    return {"x": x,
            "w_reduce_words": w_reduce_words,
            "w_reduce_scales": w_reduce_scales,
            "b_reduce": b_reduce,
            "w_span_words": w_span_words,
            "w_span_scales": w_span_scales,
            "b_span": b_span}


def reference(x, w_reduce_words, w_reduce_scales, b_reduce, w_span_words, w_span_scales, b_span):
    x = f64(x)
    red = np.maximum((unpack_weight(w_reduce_words, w_reduce_scales, FMT).T @ mxq(x.reshape(B, C, H * W), 1, "e4m3")) + f64(b_reduce)[None, :, None], 0.0)
    kern = (unpack_weight(w_span_words, w_span_scales, FMT).T @ mxq(red, 1, "e4m3")) + f64(b_span)[None, :, None]
    kern = kern.reshape(B, G, KK, H, W)
    e = np.exp(kern - kern.max(axis=2, keepdims=True))
    kern = e / e.sum(axis=2, keepdims=True)
    xp = np.pad(x, ((0, 0), (0, 0), (PAD, PAD), (PAD, PAD)))
    xg = xp.reshape(B, G, C // G, H + 2 * PAD, W + 2 * PAD)
    out = np.zeros((B, G, C // G, H, W))
    for i in range(K):
        for j in range(K):
            out = out + kern[:, :, None, i * K + j] * xg[:, :, :, i:i + H, j:j + W]
    return out.reshape(B, C, H, W)

@@ -1,0 +1,372 @@
+from contextlib import ExitStack
+
+import concourse.mybir as mybir
+from concourse.masks import make_identity
+
+BF16 = mybir.dt.bfloat16
+F32 = mybir.dt.float32
+I32 = mybir.dt.int32
+U32 = mybir.dt.uint32
+U8 = mybir.dt.uint8
+FP8X4 = mybir.dt.float8_e4m3fn_x4
+ALU = mybir.AluOpType
+ACT = mybir.ActivationFunctionType
+AXIS_X = mybir.AxisListType.X
+
+P = 128
+PACK = 4
+K_PASS = P * PACK
+BANK_F32 = 512
+BANK_BF16 = 1024
+
+C, H, W = 1024, 8, 16
+PIX = H * W
+R = 8192
+GROUPS = 128
+CH_PER_GROUP = C // GROUPS
+K = 5
+PAD = K // 2
+TAPS = K * K
+O = GROUPS * TAPS
+
+C_PASSES = C // K_PASS
+R_PASSES = R // K_PASS
+C_TILES = C // P
+PAIR_TILES = C // (2 * P)
+GROUPS_PER_TILE = P // CH_PER_GROUP
+
+STREAM_WORDS = 2048
+STREAM_BUFS = 8
+REDUCE_CHUNK = STREAM_WORDS // C_PASSES
+REDUCE_CHUNKS = R // REDUCE_CHUNK
+TILES_PER_CHUNK = REDUCE_CHUNK // BANK_F32
+
+SPAN_BLOCKS = [BANK_F32] * (O // BANK_F32) + [O % BANK_F32]
+
+PLANES_PER_TILE = 4
+QUADRANTS = 4
+ROWS_PER_QUADRANT = 4
+REDUCE_PLANE_COLS = R * C_PASSES // PLANES_PER_TILE
+
+SPAN_BIAS_COLS = 4 * BANK_BF16
+BIAS_COLS = R + SPAN_BIAS_COLS
+
+MAX_GROUPS = BANK_F32 // TAPS + 1
+
+FLAT_PAD = PAD * W + PAD
+FLAT = FLAT_PAD + PIX + FLAT_PAD
+
+SCRATCH_BANKS = 4
+ACC_BANKS = 3
+
+FLOPS = 2 * PIX * (C * R + R * O) + 2 * TAPS * C * PIX
+
+
+def tile_involution_k_kernel(
+    tc, x, w_reduce_words, w_reduce_scales, b_reduce, w_span_words, w_span_scales, b_span, out
+):
+    nc = tc.nc
+    image = x[0]
+    out_rows = out[0].rearrange("c h w -> c (h w)")
+    reduce_bytes = w_reduce_words.rearrange("g p n t -> p g (n t)")
+    span_bytes = w_span_words.rearrange("g p n t -> p g (n t)")
+
+    with ExitStack() as ctx:
+        keep = ctx.enter_context(tc.tile_pool(name="keep", bufs=1))
+        stream = ctx.enter_context(tc.tile_pool(name="stream", bufs=STREAM_BUFS))
+        psum = ctx.enter_context(tc.psum_pool(name="psum", bufs=1))
+
+        ident_bf16 = keep.tile([P, P], BF16)
+        ident_f32 = keep.tile([P, P], F32)
+        ones = keep.tile([P, P], BF16)
+        reduce_planes = keep.tile([P, REDUCE_PLANE_COLS], U8, align_bytes=64)
+        span_planes = keep.tile([P, R_PASSES // PLANES_PER_TILE, O], U8, align_bytes=64)
+        x_codes = keep.tile([P, C_PASSES, PIX], U32, align_bytes=64)
+        x_scales = keep.tile([P, C_PASSES, PIX], U8, align_bytes=64)
+        red_codes = keep.tile([P, R_PASSES, PIX], U32, align_bytes=64)
+        red_scales = keep.tile([P, R_PASSES, PIX], U8, align_bytes=64)
+        span_bias = keep.tile([P, SPAN_BIAS_COLS], BF16)
+        shifted = keep.tile([P, TAPS, C], BF16)
+        kern = keep.tile([P, O], F32)
+
+        with tc.tile_pool(name="early", bufs=1) as early:
+            make_identity(nc, ident_f32[:])
+            make_identity(nc, ident_bf16[:])
+            nc.vector.memset(ones[:], 1.0)
+
+            x_pairs = early.tile([P, PAIR_TILES, 2, PIX], BF16)
+            nc.scalar.dma_start(
+                out=x_pairs[:], in_=image.rearrange("(pt k e) h w -> k pt e (h w)", k=P, e=2)
+            )
+            x_by_word = early.tile([P, C_PASSES, PACK, PIX], BF16)
+            nc.scalar.dma_start(
+                out=x_by_word[:], in_=image.rearrange("(g p t) h w -> p g t (h w)", p=P, t=PACK)
+            )
+            bias_row = early.tile([P, BIAS_COLS], BF16)
+            nc.gpsimd.memset(bias_row[:].bitcast(F32), 0.0)
+            nc.scalar.dma_start(out=bias_row[0:1, 0:R], in_=b_reduce.rearrange("(o r) -> o r", o=1))
+            nc.scalar.dma_start(out=bias_row[0:1, R : R + O], in_=b_span.rearrange("(o r) -> o r", o=1))
+
+            nc.vector.memset(reduce_planes[:].bitcast(I32), 0)
+            for quadrant in range(QUADRANTS):
+                for half in range(2):
+                    first_row = 32 * quadrant + 8 * half
+                    nc.sync.dma_start(
+                        out=reduce_planes[first_row : first_row + 8, :].bitcast(I32),
+                        in_=w_reduce_scales[
+                            :,
+                            ROWS_PER_QUADRANT * quadrant : ROWS_PER_QUADRANT * (quadrant + 1),
+                            REDUCE_PLANE_COLS * half : REDUCE_PLANE_COLS * (half + 1),
+                        ].bitcast(I32),
+                    )
+            reduce_words = []
+            for chunk in range(REDUCE_CHUNKS):
+                words = stream.tile(
+                    [P, STREAM_WORDS], U32, tag="words", name="reduce_words", align_bytes=64
+                )
+                nc.sync.dma_start(
+                    out=words[:].rearrange("p (g n) -> p g n", g=C_PASSES).bitcast(I32),
+                    in_=reduce_bytes[
+                        :, :, PACK * REDUCE_CHUNK * chunk : PACK * REDUCE_CHUNK * (chunk + 1)
+                    ].bitcast(I32),
+                )
+                reduce_words.append(words)
+
+            x_masked = early.tile([P, K, PAIR_TILES, FLAT], F32)
+            nc.vector.memset(x_masked[:], 0.0)
+            x_words = early.tile([P, PAIR_TILES, PIX, 2], BF16)
+            nc.vector.tensor_copy(out=x_words[:], in_=x_pairs[:].rearrange("k pt e n -> k pt n e"))
+            for j in range(K):
+                lo = max(0, j - PAD)
+                hi = W + min(0, j - PAD)
+                nc.vector.tensor_copy(
+                    out=x_masked[:, j, :, FLAT_PAD : FLAT_PAD + PIX].rearrange(
+                        "k pt (h w) -> k pt h w", w=W
+                    )[:, :, :, lo:hi],
+                    in_=x_words[:]
+                    .rearrange("k pt n e -> k pt (n e)")
+                    .bitcast(F32)
+                    .rearrange("k pt (h w) -> k pt h w", w=W)[:, :, :, lo:hi],
+                )
+            for tap in range(TAPS):
+                i, j = divmod(tap, K)
+                first = FLAT_PAD + (i - PAD) * W + (j - PAD)
+                window = psum.tile([P, PAIR_TILES, P], F32, tag="scratch", bufs=SCRATCH_BANKS)
+                for pt in range(PAIR_TILES):
+                    nc.tensor.transpose(
+                        window[:, pt, :], x_masked[:, j, pt, first : first + PIX], ident_f32[:]
+                    )
+                copy_out = nc.scalar.copy if tap % 2 == 0 else nc.vector.tensor_copy
+                copy_out(
+                    out=shifted[:, tap, :].bitcast(F32), in_=window[:].rearrange("p pt k -> p (pt k)")
+                )
+
+            x_grouped = early.tile([P, C_PASSES, PIX, PACK], BF16, align_bytes=64)
+            nc.vector.tensor_copy(out=x_grouped[:], in_=x_by_word[:].rearrange("p g t n -> p g n t"))
+            nc.vector.quantize_mx(
+                out=x_codes[:].rearrange("p g n -> p (g n)").bitcast(FP8X4),
+                scales=x_scales[:].rearrange("p g n -> p (g n)"),
+                in_=x_grouped[:].rearrange("p g n t -> p (g n t)"),
+            )
+
+            nc.vector.memset(span_planes[:].rearrange("p a n -> p (a n)").bitcast(I32), 0)
+            for slab in range(R_PASSES // PLANES_PER_TILE):
+                for quadrant in range(QUADRANTS):
+                    nc.sync.dma_start(
+                        out=span_planes[32 * quadrant : 32 * quadrant + 16, slab, :].bitcast(I32),
+                        in_=w_span_scales[
+                            PLANES_PER_TILE * slab : PLANES_PER_TILE * (slab + 1),
+                            ROWS_PER_QUADRANT * quadrant : ROWS_PER_QUADRANT * (quadrant + 1),
+                            :,
+                        ].bitcast(I32),
+                    )
+
+            def broadcast_bias(first_col, dest):
+                bank = psum.tile([P, BANK_BF16], BF16, tag="scratch", bufs=SCRATCH_BANKS, name="bias_bank")
+                for half in range(BANK_BF16 // BANK_F32):
+                    nc.tensor.matmul(
+                        out=bank[:, BANK_F32 * half : BANK_F32 * (half + 1)],
+                        lhsT=ones[:],
+                        rhs=bias_row[:, first_col + BANK_F32 * half : first_col + BANK_F32 * (half + 1)],
+                        start=True,
+                        stop=True,
+                    )
+                nc.scalar.copy(out=dest, in_=bank[:])
+
+            def reduce_product(chunk):
+                reduce_bias = early.tile([P, REDUCE_CHUNK], BF16, bufs=2)
+                broadcast_bias(REDUCE_CHUNK * chunk, reduce_bias[:])
+                biased = early.tile([P, TILES_PER_CHUNK, PACK, P], BF16, bufs=2)
+                for a in range(TILES_PER_CHUNK):
+                    first_r = REDUCE_CHUNK * chunk + BANK_F32 * a
+                    half, plane_col = divmod(first_r, REDUCE_PLANE_COLS)
+                    acc = psum.tile([P, BANK_F32], F32, tag="acc", bufs=ACC_BANKS)
+                    for g in range(C_PASSES):
+                        first_word = REDUCE_CHUNK * g + BANK_F32 * a
+                        nc.tensor.matmul_mx(
+                            out=acc[:],
+                            lhsT=x_codes[:, g, :].bitcast(FP8X4),
+                            lhsT_scale=x_scales[:, g, :],
+                            rhs=reduce_words[chunk][:, first_word : first_word + BANK_F32].bitcast(FP8X4),
+                            rhs_scale=reduce_planes[
+                                ROWS_PER_QUADRANT * (2 * half + g) : P, plane_col : plane_col + BANK_F32
+                            ],
+                            start=(g == 0),
+                            stop=(g == C_PASSES - 1),
+                        )
+                    nc.vector.tensor_tensor(
+                        out=biased[:, a, :, :],
+                        in0=acc[:].rearrange("p (q t) -> p t q", t=PACK),
+                        in1=reduce_bias[:, BANK_F32 * a : BANK_F32 * (a + 1)].rearrange(
+                            "p (q t) -> p t q", t=PACK
+                        ),
+                        op=ALU.add,
+                    )
+                return biased
+
+            def quantise_red(chunk, biased):
+                flipped = psum.tile(
+                    [P, TILES_PER_CHUNK, PACK, PIX], BF16, tag="scratch", bufs=SCRATCH_BANKS
+                )
+                for a in range(TILES_PER_CHUNK):
+                    for t in range(PACK):
+                        nc.tensor.transpose(flipped[:, a, t, :], biased[:, a, t, :], ident_bf16[:])
+                red_grouped = early.tile([P, TILES_PER_CHUNK, PIX, PACK], BF16, bufs=2, align_bytes=64)
+                nc.scalar.activation(
+                    out=red_grouped[:], in_=flipped[:].rearrange("q a t n -> q a n t"), func=ACT.Relu
+                )
+                passes = slice(TILES_PER_CHUNK * chunk, TILES_PER_CHUNK * (chunk + 1))
+                nc.vector.quantize_mx(
+                    out=red_codes[:, passes, :].rearrange("q a n -> q (a n)").bitcast(FP8X4),
+                    scales=red_scales[:, passes, :].rearrange("q a n -> q (a n)"),
+                    in_=red_grouped[:].rearrange("q a n t -> q (a n t)"),
+                )
+
+            biased_ahead = reduce_product(0)
+            for chunk in range(REDUCE_CHUNKS):
+                biased_now = biased_ahead
+                if chunk + 1 < REDUCE_CHUNKS:
+                    biased_ahead = reduce_product(chunk + 1)
+                quantise_red(chunk, biased_now)
+
+            for piece in range(SPAN_BIAS_COLS // BANK_BF16):
+                broadcast_bias(
+                    R + BANK_BF16 * piece, span_bias[:, BANK_BF16 * piece : BANK_BF16 * (piece + 1)]
+                )
+
+        late = ctx.enter_context(tc.tile_pool(name="late", bufs=2))
+        products = {}
+
+        def span_product(first_col, width):
+            cols = slice(first_col, first_col + width)
+            passes_per_load = STREAM_WORDS // width
+            acc = psum.tile([P, BANK_F32], F32, tag="acc", bufs=ACC_BANKS)
+            for first_pass in range(0, R_PASSES, passes_per_load):
+                words = stream.tile(
+                    [P, STREAM_WORDS], U32, tag="words", name="span_words", align_bytes=64
+                )
+                nc.sync.dma_start(
+                    out=words[:].rearrange("p (g n) -> p g n", n=width).bitcast(I32),
+                    in_=span_bytes[
+                        :,
+                        first_pass : first_pass + passes_per_load,
+                        PACK * first_col : PACK * (first_col + width),
+                    ].bitcast(I32),
+                )
+                for g in range(first_pass, first_pass + passes_per_load):
+                    first_word = width * (g - first_pass)
+                    nc.tensor.matmul_mx(
+                        out=acc[:, :width],
+                        lhsT=red_codes[:, g, :].bitcast(FP8X4),
+                        lhsT_scale=red_scales[:, g, :],
+                        rhs=words[:, first_word : first_word + width].bitcast(FP8X4),
+                        rhs_scale=span_planes[
+                            ROWS_PER_QUADRANT * (g % PLANES_PER_TILE) : P, g // PLANES_PER_TILE, cols
+                        ],
+                        start=(g == 0),
+                        stop=(g == R_PASSES - 1),
+                    )
+            return acc
+
+        def softmax(first_group, end_group):
+            n = end_group - first_group
+            logits = kern[:, TAPS * first_group : TAPS * end_group].rearrange("p (g t) -> p g t", t=TAPS)
+            top = late.tile([P, MAX_GROUPS], F32)
+            nc.vector.tensor_reduce(out=top[:, :n], in_=logits, axis=AXIS_X, op=ALU.max)
+            centred = late.tile([P, MAX_GROUPS, TAPS], F32)
+            nc.vector.tensor_tensor(
+                out=centred[:, :n, :],
+                in0=logits,
+                in1=top[:, :n].unsqueeze(2).to_broadcast([P, n, TAPS]),
+                op=ALU.subtract,
+            )
+            expd = late.tile([P, MAX_GROUPS, TAPS], F32)
+            nc.scalar.activation(out=expd[:, :n, :], in_=centred[:, :n, :], func=ACT.Exp)
+            total = late.tile([P, MAX_GROUPS], F32)
+            nc.vector.tensor_reduce(out=total[:, :n], in_=expd[:, :n, :], axis=AXIS_X, op=ALU.add)
+            inverse = late.tile([P, MAX_GROUPS], F32)
+            nc.vector.reciprocal(out=inverse[:, :n], in_=total[:, :n])
+            prob = late.tile([P, MAX_GROUPS, TAPS], F32)
+            nc.vector.tensor_tensor(
+                out=prob[:, :n, :],
+                in0=expd[:, :n, :],
+                in1=inverse[:, :n].unsqueeze(2).to_broadcast([P, n, TAPS]),
+                op=ALU.mult,
+            )
+            return prob
+
+        def multiply(prob, prob_first_group, first_group, end_group):
+            n = end_group - first_group
+            c_tile = first_group // GROUPS_PER_TILE
+            first_channel = CH_PER_GROUP * first_group
+            end_channel = CH_PER_GROUP * end_group
+            nc.vector.tensor_tensor(
+                out=products[c_tile][:, :, first_channel - P * c_tile : end_channel - P * c_tile].rearrange(
+                    "p t (g c) -> p t g c", c=CH_PER_GROUP
+                ),
+                in0=shifted[:, :, first_channel:end_channel].rearrange("p t (g c) -> p t g c", c=CH_PER_GROUP),
+                in1=prob[:, first_group - prob_first_group : end_group - prob_first_group, :]
+                .rearrange("p g t -> p t g")
+                .unsqueeze(3)
+                .to_broadcast([P, TAPS, n, CH_PER_GROUP]),
+                op=ALU.mult,
+            )
+
+        def add_taps_and_store(c_tile):
+            summed = psum.tile([P, PIX], F32, tag="summed", bufs=1)
+            for tap in range(TAPS):
+                nc.tensor.matmul(
+                    out=summed[:],
+                    lhsT=products[c_tile][:, tap, :],
+                    rhs=ident_f32[:],
+                    start=(tap == 0),
+                    stop=(tap == TAPS - 1),
+                    is_transpose=True,
+                )
+            result = late.tile([P, PIX], F32)
+            nc.scalar.copy(out=result[:], in_=summed[:])
+            nc.scalar.dma_start(out=out_rows[P * c_tile : P * (c_tile + 1), :], in_=result[:])
+
+        block_starts = [sum(SPAN_BLOCKS[:b]) for b in range(len(SPAN_BLOCKS))]
+        groups_done = 0
+        acc_ahead = span_product(block_starts[0], SPAN_BLOCKS[0])
+        for b, width in enumerate(SPAN_BLOCKS):
+            acc_now = acc_ahead
+            if b + 1 < len(SPAN_BLOCKS):
+                acc_ahead = span_product(block_starts[b + 1], SPAN_BLOCKS[b + 1])
+            cols = slice(block_starts[b], block_starts[b] + width)
+            nc.vector.tensor_tensor(
+                out=kern[:, cols], in0=acc_now[:, :width], in1=span_bias[:, cols], op=ALU.add
+            )
+            groups_ready = (block_starts[b] + width) // TAPS
+            prob_first_group = groups_done
+            prob = softmax(prob_first_group, groups_ready)
+            while groups_done < groups_ready:
+                c_tile = groups_done // GROUPS_PER_TILE
+                end_group = min(groups_ready, GROUPS_PER_TILE * (c_tile + 1))
+                if groups_done == GROUPS_PER_TILE * c_tile:
+                    products[c_tile] = late.tile([P, TAPS, P], F32, name="products")
+                multiply(prob, prob_first_group, groups_done, end_group)
+                groups_done = end_group
+                if groups_done == GROUPS_PER_TILE * (c_tile + 1):
+                    add_taps_and_store(c_tile)

@@ -58,6 +58,7 @@ FLAT = FLAT_PAD + PIX + FLAT_PAD
 
 SCRATCH_BANKS = 4
 ACC_BANKS = 3
+PRODUCT_BUFS = 3
 
 FLOPS = 2 * PIX * (C * R + R * O) + 2 * TAPS * C * PIX
 
@@ -75,6 +76,7 @@ def tile_involution_k_kernel(
         keep = ctx.enter_context(tc.tile_pool(name="keep", bufs=1))
         stream = ctx.enter_context(tc.tile_pool(name="stream", bufs=STREAM_BUFS))
         psum = ctx.enter_context(tc.psum_pool(name="psum", bufs=1))
+        ctx.enter_context(tc.manual_schedule())
 
         ident_bf16 = keep.tile([P, P], BF16)
         ident_f32 = keep.tile([P, P], F32)
@@ -94,6 +96,8 @@ def tile_involution_k_kernel(
             make_identity(nc, ident_bf16[:])
             nc.vector.memset(ones[:], 1.0)
 
+            nc.vector.memset(reduce_planes[:].bitcast(I32), 0)
+
             x_pairs = early.tile([P, PAIR_TILES, 2, PIX], BF16)
             nc.scalar.dma_start(
                 out=x_pairs[:], in_=image.rearrange("(pt k e) h w -> k pt e (h w)", k=P, e=2)
@@ -103,11 +107,10 @@ def tile_involution_k_kernel(
                 out=x_by_word[:], in_=image.rearrange("(g p t) h w -> p g t (h w)", p=P, t=PACK)
             )
             bias_row = early.tile([P, BIAS_COLS], BF16)
-            nc.gpsimd.memset(bias_row[:].bitcast(F32), 0.0)
+            nc.vector.memset(bias_row[:].bitcast(I32), 0)
             nc.scalar.dma_start(out=bias_row[0:1, 0:R], in_=b_reduce.rearrange("(o r) -> o r", o=1))
             nc.scalar.dma_start(out=bias_row[0:1, R : R + O], in_=b_span.rearrange("(o r) -> o r", o=1))
 
-            nc.vector.memset(reduce_planes[:].bitcast(I32), 0)
             for quadrant in range(QUADRANTS):
                 for half in range(2):
                     first_row = 32 * quadrant + 8 * half
@@ -133,7 +136,8 @@ def tile_involution_k_kernel(
                 reduce_words.append(words)
 
             x_masked = early.tile([P, K, PAIR_TILES, FLAT], F32)
-            nc.vector.memset(x_masked[:], 0.0)
+            nc.gpsimd.memset(x_masked[:], 0.0)
+            nc.gpsimd.memset(span_planes[:].rearrange("p a n -> p (a n)").bitcast(F32), 0.0)
             x_words = early.tile([P, PAIR_TILES, PIX, 2], BF16)
             nc.vector.tensor_copy(out=x_words[:], in_=x_pairs[:].rearrange("k pt e n -> k pt n e"))
             for j in range(K):
@@ -148,6 +152,14 @@ def tile_involution_k_kernel(
                     .bitcast(F32)
                     .rearrange("k pt (h w) -> k pt h w", w=W)[:, :, :, lo:hi],
                 )
+            x_grouped = early.tile([P, C_PASSES, PIX, PACK], BF16, align_bytes=64)
+            nc.vector.tensor_copy(out=x_grouped[:], in_=x_by_word[:].rearrange("p g t n -> p g n t"))
+            nc.vector.quantize_mx(
+                out=x_codes[:].rearrange("p g n -> p (g n)").bitcast(FP8X4),
+                scales=x_scales[:].rearrange("p g n -> p (g n)"),
+                in_=x_grouped[:].rearrange("p g n t -> p (g n t)"),
+            )
+
             for tap in range(TAPS):
                 i, j = divmod(tap, K)
                 first = FLAT_PAD + (i - PAD) * W + (j - PAD)
@@ -161,15 +173,6 @@ def tile_involution_k_kernel(
                     out=shifted[:, tap, :].bitcast(F32), in_=window[:].rearrange("p pt k -> p (pt k)")
                 )
 
-            x_grouped = early.tile([P, C_PASSES, PIX, PACK], BF16, align_bytes=64)
-            nc.vector.tensor_copy(out=x_grouped[:], in_=x_by_word[:].rearrange("p g t n -> p g n t"))
-            nc.vector.quantize_mx(
-                out=x_codes[:].rearrange("p g n -> p (g n)").bitcast(FP8X4),
-                scales=x_scales[:].rearrange("p g n -> p (g n)"),
-                in_=x_grouped[:].rearrange("p g n t -> p (g n t)"),
-            )
-
-            nc.vector.memset(span_planes[:].rearrange("p a n -> p (a n)").bitcast(I32), 0)
             for slab in range(R_PASSES // PLANES_PER_TILE):
                 for quadrant in range(QUADRANTS):
                     nc.sync.dma_start(
@@ -332,8 +335,8 @@ def tile_involution_k_kernel(
                 op=ALU.mult,
             )
 
-        def add_taps_and_store(c_tile):
-            summed = psum.tile([P, PIX], F32, tag="summed", bufs=1)
+        def add_taps(c_tile):
+            summed = psum.tile([P, PIX], F32, tag="scratch", bufs=SCRATCH_BANKS)
             for tap in range(TAPS):
                 nc.tensor.matmul(
                     out=summed[:],
@@ -343,14 +346,19 @@ def tile_involution_k_kernel(
                     stop=(tap == TAPS - 1),
                     is_transpose=True,
                 )
+            return summed
+
+        def store(c_tile, summed):
             result = late.tile([P, PIX], F32)
             nc.scalar.copy(out=result[:], in_=summed[:])
             nc.scalar.dma_start(out=out_rows[P * c_tile : P * (c_tile + 1), :], in_=result[:])
 
         block_starts = [sum(SPAN_BLOCKS[:b]) for b in range(len(SPAN_BLOCKS))]
         groups_done = 0
+        finished = []
         acc_ahead = span_product(block_starts[0], SPAN_BLOCKS[0])
         for b, width in enumerate(SPAN_BLOCKS):
+            sums = [add_taps(c_tile) for c_tile in finished]
             acc_now = acc_ahead
             if b + 1 < len(SPAN_BLOCKS):
                 acc_ahead = span_product(block_starts[b + 1], SPAN_BLOCKS[b + 1])
@@ -361,12 +369,17 @@ def tile_involution_k_kernel(
             groups_ready = (block_starts[b] + width) // TAPS
             prob_first_group = groups_done
             prob = softmax(prob_first_group, groups_ready)
+            for c_tile, summed in zip(finished, sums):
+                store(c_tile, summed)
+            finished = []
             while groups_done < groups_ready:
                 c_tile = groups_done // GROUPS_PER_TILE
                 end_group = min(groups_ready, GROUPS_PER_TILE * (c_tile + 1))
                 if groups_done == GROUPS_PER_TILE * c_tile:
-                    products[c_tile] = late.tile([P, TAPS, P], F32, name="products")
+                    products[c_tile] = late.tile([P, TAPS, P], F32, name="products", bufs=PRODUCT_BUFS)
                 multiply(prob, prob_first_group, groups_done, end_group)
                 groups_done = end_group
                 if groups_done == GROUPS_PER_TILE * (c_tile + 1):
-                    add_taps_and_store(c_tile)
+                    finished.append(c_tile)
+        for c_tile in finished:
+            store(c_tile, add_taps(c_tile))

@@ -41,15 +41,17 @@ REDUCE_CHUNK = STREAM_WORDS // C_PASSES
 REDUCE_CHUNKS = R // REDUCE_CHUNK
 TILES_PER_CHUNK = REDUCE_CHUNK // BANK_F32
 
-SPAN_BLOCKS = [BANK_F32] * (O // BANK_F32) + [O % BANK_F32]
+SPAN_BLOCKS = [512, 512, 512, 512, 512, 256, 256, 128]
+PASSES_PER_LOAD = 4
 
 PLANES_PER_TILE = 4
 QUADRANTS = 4
 ROWS_PER_QUADRANT = 4
 REDUCE_PLANE_COLS = R * C_PASSES // PLANES_PER_TILE
 
-SPAN_BIAS_COLS = 4 * BANK_BF16
-BIAS_COLS = R + SPAN_BIAS_COLS
+REDUCE_BIAS_ROWS = R // P
+SPAN_BIAS_ROWS = O // P
+ROWS_PER_BANK = BANK_BF16 // P
 
 MAX_GROUPS = BANK_F32 // TAPS + 1
 
@@ -58,7 +60,7 @@ FLAT = FLAT_PAD + PIX + FLAT_PAD
 
 SCRATCH_BANKS = 4
 ACC_BANKS = 3
-PRODUCT_BUFS = 3
+PRODUCT_BUFS = 4
 
 FLOPS = 2 * PIX * (C * R + R * O) + 2 * TAPS * C * PIX
 
@@ -80,21 +82,19 @@ def tile_involution_k_kernel(
 
         ident_bf16 = keep.tile([P, P], BF16)
         ident_f32 = keep.tile([P, P], F32)
-        ones = keep.tile([P, P], BF16)
         reduce_planes = keep.tile([P, REDUCE_PLANE_COLS], U8, align_bytes=64)
         span_planes = keep.tile([P, R_PASSES // PLANES_PER_TILE, O], U8, align_bytes=64)
         x_codes = keep.tile([P, C_PASSES, PIX], U32, align_bytes=64)
         x_scales = keep.tile([P, C_PASSES, PIX], U8, align_bytes=64)
         red_codes = keep.tile([P, R_PASSES, PIX], U32, align_bytes=64)
         red_scales = keep.tile([P, R_PASSES, PIX], U8, align_bytes=64)
-        span_bias = keep.tile([P, SPAN_BIAS_COLS], BF16)
+        span_bias = keep.tile([P, O], BF16)
         shifted = keep.tile([P, TAPS, C], BF16)
         kern = keep.tile([P, O], F32)
 
         with tc.tile_pool(name="early", bufs=1) as early:
             make_identity(nc, ident_f32[:])
             make_identity(nc, ident_bf16[:])
-            nc.vector.memset(ones[:], 1.0)
 
             nc.vector.memset(reduce_planes[:].bitcast(I32), 0)
 
@@ -106,10 +106,15 @@ def tile_involution_k_kernel(
             nc.scalar.dma_start(
                 out=x_by_word[:], in_=image.rearrange("(g p t) h w -> p g t (h w)", p=P, t=PACK)
             )
-            bias_row = early.tile([P, BIAS_COLS], BF16)
-            nc.vector.memset(bias_row[:].bitcast(I32), 0)
-            nc.scalar.dma_start(out=bias_row[0:1, 0:R], in_=b_reduce.rearrange("(o r) -> o r", o=1))
-            nc.scalar.dma_start(out=bias_row[0:1, R : R + O], in_=b_span.rearrange("(o r) -> o r", o=1))
+            bias_rows = early.tile([P, P], BF16)
+            nc.vector.memset(bias_rows[:], 0.0)
+            nc.scalar.dma_start(
+                out=bias_rows[0:REDUCE_BIAS_ROWS, :], in_=b_reduce.rearrange("(m n) -> m n", n=P)
+            )
+            nc.scalar.dma_start(
+                out=bias_rows[REDUCE_BIAS_ROWS : REDUCE_BIAS_ROWS + SPAN_BIAS_ROWS, :],
+                in_=b_span.rearrange("(m n) -> m n", n=P),
+            )
 
             for quadrant in range(QUADRANTS):
                 for half in range(2):
@@ -160,6 +165,28 @@ def tile_involution_k_kernel(
                 in_=x_grouped[:].rearrange("p g n t -> p (g n t)"),
             )
 
+            bias_cols = early.tile([P, P], BF16)
+            bias_flipped = psum.tile([P, P], BF16, tag="scratch", bufs=SCRATCH_BANKS)
+            nc.tensor.transpose(bias_flipped[:], bias_rows[:], ident_bf16[:])
+            nc.scalar.copy(out=bias_cols[:], in_=bias_flipped[:])
+            reduce_bias = early.tile([P, R], BF16)
+
+            def broadcast_bias(first_row, rows, dest):
+                bank = psum.tile([P, BANK_BF16], BF16, tag="scratch", bufs=SCRATCH_BANKS, name="bias_bank")
+                for s in range(rows):
+                    nc.tensor.matmul(
+                        out=bank[:, P * s : P * (s + 1)],
+                        lhsT=bias_cols[:, first_row + s : first_row + s + 1].to_broadcast([P, P]),
+                        rhs=ident_bf16[:],
+                        start=True,
+                        stop=True,
+                    )
+                nc.scalar.copy(out=dest, in_=bank[:, : P * rows])
+
+            bias_banks = [
+                (first_row, min(ROWS_PER_BANK, REDUCE_BIAS_ROWS + SPAN_BIAS_ROWS - first_row))
+                for first_row in range(0, REDUCE_BIAS_ROWS + SPAN_BIAS_ROWS, ROWS_PER_BANK)
+            ]
             for tap in range(TAPS):
                 i, j = divmod(tap, K)
                 first = FLAT_PAD + (i - PAD) * W + (j - PAD)
@@ -172,6 +199,14 @@ def tile_involution_k_kernel(
                 copy_out(
                     out=shifted[:, tap, :].bitcast(F32), in_=window[:].rearrange("p pt k -> p (pt k)")
                 )
+                if tap % 2 == 1:
+                    first_row, rows = bias_banks[tap // 2]
+                    if first_row < REDUCE_BIAS_ROWS:
+                        dest = reduce_bias[:, P * first_row : P * (first_row + rows)]
+                    else:
+                        first_span_row = first_row - REDUCE_BIAS_ROWS
+                        dest = span_bias[:, P * first_span_row : P * (first_span_row + rows)]
+                    broadcast_bias(first_row, rows, dest)
 
             for slab in range(R_PASSES // PLANES_PER_TILE):
                 for quadrant in range(QUADRANTS):
@@ -184,21 +219,7 @@ def tile_involution_k_kernel(
                         ].bitcast(I32),
                     )
 
-            def broadcast_bias(first_col, dest):
-                bank = psum.tile([P, BANK_BF16], BF16, tag="scratch", bufs=SCRATCH_BANKS, name="bias_bank")
-                for half in range(BANK_BF16 // BANK_F32):
-                    nc.tensor.matmul(
-                        out=bank[:, BANK_F32 * half : BANK_F32 * (half + 1)],
-                        lhsT=ones[:],
-                        rhs=bias_row[:, first_col + BANK_F32 * half : first_col + BANK_F32 * (half + 1)],
-                        start=True,
-                        stop=True,
-                    )
-                nc.scalar.copy(out=dest, in_=bank[:])
-
             def reduce_product(chunk):
-                reduce_bias = early.tile([P, REDUCE_CHUNK], BF16, bufs=2)
-                broadcast_bias(REDUCE_CHUNK * chunk, reduce_bias[:])
                 biased = early.tile([P, TILES_PER_CHUNK, PACK, P], BF16, bufs=2)
                 for a in range(TILES_PER_CHUNK):
                     first_r = REDUCE_CHUNK * chunk + BANK_F32 * a
@@ -220,7 +241,7 @@ def tile_involution_k_kernel(
                     nc.vector.tensor_tensor(
                         out=biased[:, a, :, :],
                         in0=acc[:].rearrange("p (q t) -> p t q", t=PACK),
-                        in1=reduce_bias[:, BANK_F32 * a : BANK_F32 * (a + 1)].rearrange(
+                        in1=reduce_bias[:, first_r : first_r + BANK_F32].rearrange(
                             "p (q t) -> p t q", t=PACK
                         ),
                         op=ALU.add,
@@ -252,31 +273,25 @@ def tile_involution_k_kernel(
                     biased_ahead = reduce_product(chunk + 1)
                 quantise_red(chunk, biased_now)
 
-            for piece in range(SPAN_BIAS_COLS // BANK_BF16):
-                broadcast_bias(
-                    R + BANK_BF16 * piece, span_bias[:, BANK_BF16 * piece : BANK_BF16 * (piece + 1)]
-                )
-
         late = ctx.enter_context(tc.tile_pool(name="late", bufs=2))
         products = {}
 
         def span_product(first_col, width):
             cols = slice(first_col, first_col + width)
-            passes_per_load = STREAM_WORDS // width
             acc = psum.tile([P, BANK_F32], F32, tag="acc", bufs=ACC_BANKS)
-            for first_pass in range(0, R_PASSES, passes_per_load):
+            for first_pass in range(0, R_PASSES, PASSES_PER_LOAD):
                 words = stream.tile(
                     [P, STREAM_WORDS], U32, tag="words", name="span_words", align_bytes=64
                 )
                 nc.sync.dma_start(
-                    out=words[:].rearrange("p (g n) -> p g n", n=width).bitcast(I32),
+                    out=words[:, : PASSES_PER_LOAD * width].rearrange("p (g n) -> p g n", n=width).bitcast(I32),
                     in_=span_bytes[
                         :,
-                        first_pass : first_pass + passes_per_load,
+                        first_pass : first_pass + PASSES_PER_LOAD,
                         PACK * first_col : PACK * (first_col + width),
                     ].bitcast(I32),
                 )
-                for g in range(first_pass, first_pass + passes_per_load):
+                for g in range(first_pass, first_pass + PASSES_PER_LOAD):
                     first_word = width * (g - first_pass)
                     nc.tensor.matmul_mx(
                         out=acc[:, :width],
@@ -356,12 +371,14 @@ def tile_involution_k_kernel(
         block_starts = [sum(SPAN_BLOCKS[:b]) for b in range(len(SPAN_BLOCKS))]
         groups_done = 0
         finished = []
+        unstored = []
         acc_ahead = span_product(block_starts[0], SPAN_BLOCKS[0])
         for b, width in enumerate(SPAN_BLOCKS):
-            sums = [add_taps(c_tile) for c_tile in finished]
             acc_now = acc_ahead
             if b + 1 < len(SPAN_BLOCKS):
                 acc_ahead = span_product(block_starts[b + 1], SPAN_BLOCKS[b + 1])
+            summed_now = [(c_tile, add_taps(c_tile)) for c_tile in finished]
+            finished = []
             cols = slice(block_starts[b], block_starts[b] + width)
             nc.vector.tensor_tensor(
                 out=kern[:, cols], in0=acc_now[:, :width], in1=span_bias[:, cols], op=ALU.add
@@ -369,9 +386,9 @@ def tile_involution_k_kernel(
             groups_ready = (block_starts[b] + width) // TAPS
             prob_first_group = groups_done
             prob = softmax(prob_first_group, groups_ready)
-            for c_tile, summed in zip(finished, sums):
+            for c_tile, summed in unstored:
                 store(c_tile, summed)
-            finished = []
+            unstored = summed_now
             while groups_done < groups_ready:
                 c_tile = groups_done // GROUPS_PER_TILE
                 end_group = min(groups_ready, GROUPS_PER_TILE * (c_tile + 1))
@@ -381,5 +398,7 @@ def tile_involution_k_kernel(
                 groups_done = end_group
                 if groups_done == GROUPS_PER_TILE * (c_tile + 1):
                     finished.append(c_tile)
+        for c_tile, summed in unstored:
+            store(c_tile, summed)
         for c_tile in finished:
             store(c_tile, add_taps(c_tile))

@@ -181,7 +181,7 @@ def tile_involution_k_kernel(
                         start=True,
                         stop=True,
                     )
-                nc.scalar.copy(out=dest, in_=bank[:, : P * rows])
+                nc.vector.tensor_copy(out=dest, in_=bank[:, : P * rows])
 
             bias_banks = [
                 (first_row, min(ROWS_PER_BANK, REDUCE_BIAS_ROWS + SPAN_BIAS_ROWS - first_row))
@@ -306,24 +306,45 @@ def tile_involution_k_kernel(
                     )
             return acc
 
-        def softmax(first_group, end_group):
-            n = end_group - first_group
-            logits = kern[:, TAPS * first_group : TAPS * end_group].rearrange("p (g t) -> p g t", t=TAPS)
-            top = late.tile([P, MAX_GROUPS], F32)
-            nc.vector.tensor_reduce(out=top[:, :n], in_=logits, axis=AXIS_X, op=ALU.max)
-            centred = late.tile([P, MAX_GROUPS, TAPS], F32)
+        n_blocks = len(SPAN_BLOCKS)
+        block_starts = [sum(SPAN_BLOCKS[:b]) for b in range(n_blocks)]
+        end_groups = [(block_starts[b] + SPAN_BLOCKS[b]) // TAPS for b in range(n_blocks)]
+        first_groups = [0] + end_groups[:-1]
+        accs = {}
+        exponentials = {}
+        totals = {}
+        finished = {}
+        sums = {}
+
+        def exponentiate(b):
+            cols = slice(block_starts[b], block_starts[b] + SPAN_BLOCKS[b])
             nc.vector.tensor_tensor(
-                out=centred[:, :n, :],
-                in0=logits,
-                in1=top[:, :n].unsqueeze(2).to_broadcast([P, n, TAPS]),
-                op=ALU.subtract,
+                out=kern[:, cols], in0=accs[b][:, : SPAN_BLOCKS[b]], in1=span_bias[:, cols], op=ALU.add
             )
+            n = end_groups[b] - first_groups[b]
+            logits = kern[:, TAPS * first_groups[b] : TAPS * end_groups[b]].rearrange(
+                "p (g t) -> p g t", t=TAPS
+            )
+            minus_top = late.tile([P, MAX_GROUPS], F32)
+            nc.vector.tensor_reduce(out=minus_top[:, :n], in_=logits, axis=AXIS_X, op=ALU.max, negate=True)
             expd = late.tile([P, MAX_GROUPS, TAPS], F32)
-            nc.scalar.activation(out=expd[:, :n, :], in_=centred[:, :n, :], func=ACT.Exp)
             total = late.tile([P, MAX_GROUPS], F32)
-            nc.vector.tensor_reduce(out=total[:, :n], in_=expd[:, :n, :], axis=AXIS_X, op=ALU.add)
+            for g in range(n):
+                nc.scalar.activation(
+                    out=expd[:, g, :],
+                    in_=logits[:, g, :],
+                    func=ACT.Exp,
+                    bias=minus_top[:, g : g + 1],
+                    accum_out=total[:, g : g + 1],
+                )
+            exponentials[b] = expd
+            totals[b] = total
+
+        def multiply(b):
+            n = end_groups[b] - first_groups[b]
+            expd = exponentials[b]
             inverse = late.tile([P, MAX_GROUPS], F32)
-            nc.vector.reciprocal(out=inverse[:, :n], in_=total[:, :n])
+            nc.vector.reciprocal(out=inverse[:, :n], in_=totals[b][:, :n])
             prob = late.tile([P, MAX_GROUPS, TAPS], F32)
             nc.vector.tensor_tensor(
                 out=prob[:, :n, :],
@@ -331,74 +352,59 @@ def tile_involution_k_kernel(
                 in1=inverse[:, :n].unsqueeze(2).to_broadcast([P, n, TAPS]),
                 op=ALU.mult,
             )
-            return prob
-
-        def multiply(prob, prob_first_group, first_group, end_group):
-            n = end_group - first_group
-            c_tile = first_group // GROUPS_PER_TILE
-            first_channel = CH_PER_GROUP * first_group
-            end_channel = CH_PER_GROUP * end_group
-            nc.vector.tensor_tensor(
-                out=products[c_tile][:, :, first_channel - P * c_tile : end_channel - P * c_tile].rearrange(
-                    "p t (g c) -> p t g c", c=CH_PER_GROUP
-                ),
-                in0=shifted[:, :, first_channel:end_channel].rearrange("p t (g c) -> p t g c", c=CH_PER_GROUP),
-                in1=prob[:, first_group - prob_first_group : end_group - prob_first_group, :]
-                .rearrange("p g t -> p t g")
-                .unsqueeze(3)
-                .to_broadcast([P, TAPS, n, CH_PER_GROUP]),
-                op=ALU.mult,
-            )
-
-        def add_taps(c_tile):
-            summed = psum.tile([P, PIX], F32, tag="scratch", bufs=SCRATCH_BANKS)
-            for tap in range(TAPS):
-                nc.tensor.matmul(
-                    out=summed[:],
-                    lhsT=products[c_tile][:, tap, :],
-                    rhs=ident_f32[:],
-                    start=(tap == 0),
-                    stop=(tap == TAPS - 1),
-                    is_transpose=True,
-                )
-            return summed
-
-        def store(c_tile, summed):
-            result = late.tile([P, PIX], F32)
-            nc.scalar.copy(out=result[:], in_=summed[:])
-            nc.scalar.dma_start(out=out_rows[P * c_tile : P * (c_tile + 1), :], in_=result[:])
-
-        block_starts = [sum(SPAN_BLOCKS[:b]) for b in range(len(SPAN_BLOCKS))]
-        groups_done = 0
-        finished = []
-        unstored = []
-        acc_ahead = span_product(block_starts[0], SPAN_BLOCKS[0])
-        for b, width in enumerate(SPAN_BLOCKS):
-            acc_now = acc_ahead
-            if b + 1 < len(SPAN_BLOCKS):
-                acc_ahead = span_product(block_starts[b + 1], SPAN_BLOCKS[b + 1])
-            summed_now = [(c_tile, add_taps(c_tile)) for c_tile in finished]
-            finished = []
-            cols = slice(block_starts[b], block_starts[b] + width)
-            nc.vector.tensor_tensor(
-                out=kern[:, cols], in0=acc_now[:, :width], in1=span_bias[:, cols], op=ALU.add
-            )
-            groups_ready = (block_starts[b] + width) // TAPS
-            prob_first_group = groups_done
-            prob = softmax(prob_first_group, groups_ready)
-            for c_tile, summed in unstored:
-                store(c_tile, summed)
-            unstored = summed_now
-            while groups_done < groups_ready:
-                c_tile = groups_done // GROUPS_PER_TILE
-                end_group = min(groups_ready, GROUPS_PER_TILE * (c_tile + 1))
-                if groups_done == GROUPS_PER_TILE * c_tile:
+            finished[b] = []
+            group = first_groups[b]
+            while group < end_groups[b]:
+                c_tile = group // GROUPS_PER_TILE
+                piece_end = min(end_groups[b], GROUPS_PER_TILE * (c_tile + 1))
+                if group == GROUPS_PER_TILE * c_tile:
                     products[c_tile] = late.tile([P, TAPS, P], F32, name="products", bufs=PRODUCT_BUFS)
-                multiply(prob, prob_first_group, groups_done, end_group)
-                groups_done = end_group
-                if groups_done == GROUPS_PER_TILE * (c_tile + 1):
-                    finished.append(c_tile)
-        for c_tile, summed in unstored:
-            store(c_tile, summed)
-        for c_tile in finished:
-            store(c_tile, add_taps(c_tile))
+                piece = products[c_tile][
+                    :, :, CH_PER_GROUP * group - P * c_tile : CH_PER_GROUP * piece_end - P * c_tile
+                ]
+                nc.vector.tensor_tensor(
+                    out=piece.rearrange("p t (g c) -> p t g c", c=CH_PER_GROUP),
+                    in0=shifted[:, :, CH_PER_GROUP * group : CH_PER_GROUP * piece_end].rearrange(
+                        "p t (g c) -> p t g c", c=CH_PER_GROUP
+                    ),
+                    in1=prob[:, group - first_groups[b] : piece_end - first_groups[b], :]
+                    .rearrange("p g t -> p t g")
+                    .unsqueeze(3)
+                    .to_broadcast([P, TAPS, piece_end - group, CH_PER_GROUP]),
+                    op=ALU.mult,
+                )
+                group = piece_end
+                if group == GROUPS_PER_TILE * (c_tile + 1):
+                    finished[b].append(c_tile)
+
+        def add_taps(b):
+            sums[b] = []
+            for c_tile in finished[b]:
+                summed = psum.tile([P, PIX], F32, tag="scratch", bufs=SCRATCH_BANKS)
+                for tap in range(TAPS):
+                    nc.tensor.matmul(
+                        out=summed[:],
+                        lhsT=products[c_tile][:, tap, :],
+                        rhs=ident_f32[:],
+                        start=(tap == 0),
+                        stop=(tap == TAPS - 1),
+                        is_transpose=True,
+                    )
+                sums[b].append((c_tile, summed))
+
+        def store(b):
+            for c_tile, summed in sums[b]:
+                result = late.tile([P, PIX], F32)
+                nc.scalar.copy(out=result[:], in_=summed[:])
+                nc.scalar.dma_start(out=out_rows[P * c_tile : P * (c_tile + 1), :], in_=result[:])
+
+        for step in range(n_blocks + 3):
+            if step < n_blocks:
+                accs[step] = span_product(block_starts[step], SPAN_BLOCKS[step])
+            if 0 <= step - 1 < n_blocks:
+                exponentiate(step - 1)
+            if 0 <= step - 2 < n_blocks:
+                multiply(step - 2)
+                add_taps(step - 2)
+            if 0 <= step - 3 < n_blocks:
+                store(step - 3)

@@ -27,12 +27,14 @@ CH_PER_GROUP = C // GROUPS
 K = 5
 PAD = K // 2
 TAPS = K * K
+HEAD_TAPS = 8
 O = GROUPS * TAPS
 
 C_PASSES = C // K_PASS
 R_PASSES = R // K_PASS
 C_TILES = C // P
-PAIR_TILES = C // (2 * P)
+PAIRS = PACK // 2
+PAIR_TILES = C_PASSES * PAIRS
 GROUPS_PER_TILE = P // CH_PER_GROUP
 
 STREAM_WORDS = 2048
@@ -41,25 +43,26 @@ REDUCE_CHUNK = STREAM_WORDS // C_PASSES
 REDUCE_CHUNKS = R // REDUCE_CHUNK
 TILES_PER_CHUNK = REDUCE_CHUNK // BANK_F32
 
-SPAN_BLOCKS = [512, 512, 512, 512, 512, 256, 256, 128]
-PASSES_PER_LOAD = 4
+SPAN_BLOCKS = [512, 640, 768, 512, 384, 256, 128]
+MM_WIDTHS = [512, 256, 128]
+MAX_PASSES_PER_LOAD = 8
+PART_GROUPS = 16
+HALF_TILE = PART_GROUPS // 2
+PART_BUFS = 3
 
 PLANES_PER_TILE = 4
 QUADRANTS = 4
 ROWS_PER_QUADRANT = 4
 REDUCE_PLANE_COLS = R * C_PASSES // PLANES_PER_TILE
 
-REDUCE_BIAS_ROWS = R // P
 SPAN_BIAS_ROWS = O // P
 ROWS_PER_BANK = BANK_BF16 // P
-
-MAX_GROUPS = BANK_F32 // TAPS + 1
 
 FLAT_PAD = PAD * W + PAD
 FLAT = FLAT_PAD + PIX + FLAT_PAD
 
 SCRATCH_BANKS = 4
-ACC_BANKS = 3
+ACC_BANKS = 4
 PRODUCT_BUFS = 4
 
 FLOPS = 2 * PIX * (C * R + R * O) + 2 * TAPS * C * PIX
@@ -82,10 +85,7 @@ def tile_involution_k_kernel(
 
         ident_bf16 = keep.tile([P, P], BF16)
         ident_f32 = keep.tile([P, P], F32)
-        reduce_planes = keep.tile([P, REDUCE_PLANE_COLS], U8, align_bytes=64)
         span_planes = keep.tile([P, R_PASSES // PLANES_PER_TILE, O], U8, align_bytes=64)
-        x_codes = keep.tile([P, C_PASSES, PIX], U32, align_bytes=64)
-        x_scales = keep.tile([P, C_PASSES, PIX], U8, align_bytes=64)
         red_codes = keep.tile([P, R_PASSES, PIX], U32, align_bytes=64)
         red_scales = keep.tile([P, R_PASSES, PIX], U8, align_bytes=64)
         span_bias = keep.tile([P, O], BF16)
@@ -93,27 +93,27 @@ def tile_involution_k_kernel(
         kern = keep.tile([P, O], F32)
 
         with tc.tile_pool(name="early", bufs=1) as early:
+            x_scales = early.tile([P, C_PASSES, PIX], U8, align_bytes=64)
+            x_codes = early.tile([P, C_PASSES, PIX], U32, align_bytes=64)
+            reduce_planes = early.tile([P, REDUCE_PLANE_COLS], U8, align_bytes=64)
             make_identity(nc, ident_f32[:])
             make_identity(nc, ident_bf16[:])
 
+            reduce_bias_rows = early.tile([P, K_PASS], BF16)
+            span_bias_rows = early.tile([P, P], BF16)
+            nc.vector.memset(reduce_bias_rows[:], 0.0)
+            nc.vector.memset(span_bias_rows[:], 0.0)
             nc.vector.memset(reduce_planes[:].bitcast(I32), 0)
 
-            x_pairs = early.tile([P, PAIR_TILES, 2, PIX], BF16)
-            nc.scalar.dma_start(
-                out=x_pairs[:], in_=image.rearrange("(pt k e) h w -> k pt e (h w)", k=P, e=2)
-            )
             x_by_word = early.tile([P, C_PASSES, PACK, PIX], BF16)
             nc.scalar.dma_start(
                 out=x_by_word[:], in_=image.rearrange("(g p t) h w -> p g t (h w)", p=P, t=PACK)
             )
-            bias_rows = early.tile([P, P], BF16)
-            nc.vector.memset(bias_rows[:], 0.0)
             nc.scalar.dma_start(
-                out=bias_rows[0:REDUCE_BIAS_ROWS, :], in_=b_reduce.rearrange("(m n) -> m n", n=P)
+                out=reduce_bias_rows[0:R_PASSES, :], in_=b_reduce.rearrange("(m n) -> m n", n=K_PASS)
             )
             nc.scalar.dma_start(
-                out=bias_rows[REDUCE_BIAS_ROWS : REDUCE_BIAS_ROWS + SPAN_BIAS_ROWS, :],
-                in_=b_span.rearrange("(m n) -> m n", n=P),
+                out=span_bias_rows[0:SPAN_BIAS_ROWS, :], in_=b_span.rearrange("(m n) -> m n", n=P)
             )
 
             for quadrant in range(QUADRANTS):
@@ -140,23 +140,21 @@ def tile_involution_k_kernel(
                 )
                 reduce_words.append(words)
 
-            x_masked = early.tile([P, K, PAIR_TILES, FLAT], F32)
-            nc.gpsimd.memset(x_masked[:], 0.0)
             nc.gpsimd.memset(span_planes[:].rearrange("p a n -> p (a n)").bitcast(F32), 0.0)
-            x_words = early.tile([P, PAIR_TILES, PIX, 2], BF16)
-            nc.vector.tensor_copy(out=x_words[:], in_=x_pairs[:].rearrange("k pt e n -> k pt n e"))
+
+            x_masked = keep.tile([P, K, PAIR_TILES, FLAT], F32)
+            nc.vector.memset(x_masked[:, :, :, 0:FLAT_PAD], 0.0)
+            nc.vector.memset(x_masked[:, :, :, FLAT_PAD + PIX : FLAT], 0.0)
             for j in range(K):
-                lo = max(0, j - PAD)
-                hi = W + min(0, j - PAD)
-                nc.vector.tensor_copy(
-                    out=x_masked[:, j, :, FLAT_PAD : FLAT_PAD + PIX].rearrange(
-                        "k pt (h w) -> k pt h w", w=W
-                    )[:, :, :, lo:hi],
-                    in_=x_words[:]
-                    .rearrange("k pt n e -> k pt (n e)")
-                    .bitcast(F32)
-                    .rearrange("k pt (h w) -> k pt h w", w=W)[:, :, :, lo:hi],
-                )
+                outside = slice(W + j - PAD, W) if j < PAD else slice(0, j - PAD)
+                if j != PAD:
+                    nc.vector.memset(
+                        x_masked[:, j, :, FLAT_PAD : FLAT_PAD + PIX].rearrange("p a (h w) -> p a h w", w=W)[
+                            :, :, :, outside
+                        ],
+                        0.0,
+                    )
+
             x_grouped = early.tile([P, C_PASSES, PIX, PACK], BF16, align_bytes=64)
             nc.vector.tensor_copy(out=x_grouped[:], in_=x_by_word[:].rearrange("p g t n -> p g n t"))
             nc.vector.quantize_mx(
@@ -164,49 +162,64 @@ def tile_involution_k_kernel(
                 scales=x_scales[:].rearrange("p g n -> p (g n)"),
                 in_=x_grouped[:].rearrange("p g n t -> p (g n t)"),
             )
+            for j in range(K):
+                lo = max(0, j - PAD)
+                hi = W + min(0, j - PAD)
+                for g in range(C_PASSES):
+                    nc.vector.tensor_copy(
+                        out=x_masked[:, j, PAIRS * g : PAIRS * (g + 1), FLAT_PAD : FLAT_PAD + PIX].rearrange(
+                            "p u (h w) -> p u h w", w=W
+                        )[:, :, :, lo:hi],
+                        in_=x_grouped[:, g, :, :]
+                        .rearrange("p n t -> p (n t)")
+                        .bitcast(F32)
+                        .rearrange("p (h w u) -> p u h w", w=W, u=PAIRS)[:, :, :, lo:hi],
+                    )
 
-            bias_cols = early.tile([P, P], BF16)
-            bias_flipped = psum.tile([P, P], BF16, tag="scratch", bufs=SCRATCH_BANKS)
-            nc.tensor.transpose(bias_flipped[:], bias_rows[:], ident_bf16[:])
-            nc.scalar.copy(out=bias_cols[:], in_=bias_flipped[:])
-            reduce_bias = early.tile([P, R], BF16)
+            reduce_bias = early.tile([P, R_PASSES, PACK], F32)
+            bias_flipped = psum.tile([P, PACK, P], BF16, tag="scratch", bufs=SCRATCH_BANKS)
+            for t in range(PACK):
+                nc.tensor.transpose(
+                    bias_flipped[:, t, :], reduce_bias_rows[:, t::PACK], ident_bf16[:]
+                )
+            nc.scalar.copy(
+                out=reduce_bias[:], in_=bias_flipped[:, :, 0:R_PASSES].rearrange("q t g -> q g t")
+            )
 
-            def broadcast_bias(first_row, rows, dest):
+            span_bias_cols = early.tile([P, P], BF16)
+            span_bias_flipped = psum.tile([P, P], BF16, tag="scratch", bufs=SCRATCH_BANKS)
+            nc.tensor.transpose(span_bias_flipped[:], span_bias_rows[:], ident_bf16[:])
+            nc.scalar.copy(out=span_bias_cols[:], in_=span_bias_flipped[:])
+
+            def spread_span_bias(first_row, rows):
                 bank = psum.tile([P, BANK_BF16], BF16, tag="scratch", bufs=SCRATCH_BANKS, name="bias_bank")
                 for s in range(rows):
                     nc.tensor.matmul(
                         out=bank[:, P * s : P * (s + 1)],
-                        lhsT=bias_cols[:, first_row + s : first_row + s + 1].to_broadcast([P, P]),
+                        lhsT=span_bias_cols[:, first_row + s : first_row + s + 1].to_broadcast([P, P]),
                         rhs=ident_bf16[:],
                         start=True,
                         stop=True,
                     )
-                nc.vector.tensor_copy(out=dest, in_=bank[:, : P * rows])
+                nc.scalar.copy(
+                    out=span_bias[:, P * first_row : P * (first_row + rows)], in_=bank[:, : P * rows]
+                )
 
-            bias_banks = [
-                (first_row, min(ROWS_PER_BANK, REDUCE_BIAS_ROWS + SPAN_BIAS_ROWS - first_row))
-                for first_row in range(0, REDUCE_BIAS_ROWS + SPAN_BIAS_ROWS, ROWS_PER_BANK)
-            ]
-            for tap in range(TAPS):
+            def shift_image(tap):
                 i, j = divmod(tap, K)
                 first = FLAT_PAD + (i - PAD) * W + (j - PAD)
-                window = psum.tile([P, PAIR_TILES, P], F32, tag="scratch", bufs=SCRATCH_BANKS)
+                window = psum.tile([P, C_PASSES, PAIRS, P], F32, tag="scratch", bufs=SCRATCH_BANKS)
                 for pt in range(PAIR_TILES):
                     nc.tensor.transpose(
-                        window[:, pt, :], x_masked[:, j, pt, first : first + PIX], ident_f32[:]
+                        window[:, pt // PAIRS, pt % PAIRS, :],
+                        x_masked[:, j, pt, first : first + PIX],
+                        ident_f32[:],
                     )
                 copy_out = nc.scalar.copy if tap % 2 == 0 else nc.vector.tensor_copy
                 copy_out(
-                    out=shifted[:, tap, :].bitcast(F32), in_=window[:].rearrange("p pt k -> p (pt k)")
+                    out=shifted[:, tap, :].bitcast(F32).rearrange("n (g p u) -> n g p u", g=C_PASSES, u=PAIRS),
+                    in_=window[:].rearrange("n g u p -> n g p u"),
                 )
-                if tap % 2 == 1:
-                    first_row, rows = bias_banks[tap // 2]
-                    if first_row < REDUCE_BIAS_ROWS:
-                        dest = reduce_bias[:, P * first_row : P * (first_row + rows)]
-                    else:
-                        first_span_row = first_row - REDUCE_BIAS_ROWS
-                        dest = span_bias[:, P * first_span_row : P * (first_span_row + rows)]
-                    broadcast_bias(first_row, rows, dest)
 
             for slab in range(R_PASSES // PLANES_PER_TILE):
                 for quadrant in range(QUADRANTS):
@@ -220,7 +233,7 @@ def tile_involution_k_kernel(
                     )
 
             def reduce_product(chunk):
-                biased = early.tile([P, TILES_PER_CHUNK, PACK, P], BF16, bufs=2)
+                raw = early.tile([P, TILES_PER_CHUNK, BANK_F32], F32, bufs=2)
                 for a in range(TILES_PER_CHUNK):
                     first_r = REDUCE_CHUNK * chunk + BANK_F32 * a
                     half, plane_col = divmod(first_r, REDUCE_PLANE_COLS)
@@ -238,27 +251,36 @@ def tile_involution_k_kernel(
                             start=(g == 0),
                             stop=(g == C_PASSES - 1),
                         )
+                    nc.scalar.copy(
+                        out=raw[:, a, :].rearrange("p (t q) -> p t q", t=PACK),
+                        in_=acc[:].rearrange("p (q t) -> p t q", t=PACK),
+                    )
+                return raw
+
+            def flip_red(chunk, raw):
+                biased = early.tile([P, TILES_PER_CHUNK, PIX, PACK], BF16, bufs=2)
+                for a in range(TILES_PER_CHUNK):
+                    flipped = psum.tile([P, PACK, PIX], F32, tag="scratch", bufs=SCRATCH_BANKS)
+                    for t in range(PACK):
+                        nc.tensor.transpose(
+                            flipped[:, t, :], raw[:, a, P * t : P * (t + 1)], ident_f32[:]
+                        )
                     nc.vector.tensor_tensor(
                         out=biased[:, a, :, :],
-                        in0=acc[:].rearrange("p (q t) -> p t q", t=PACK),
-                        in1=reduce_bias[:, first_r : first_r + BANK_F32].rearrange(
-                            "p (q t) -> p t q", t=PACK
-                        ),
+                        in0=flipped[:].rearrange("q t n -> q n t"),
+                        in1=reduce_bias[:, TILES_PER_CHUNK * chunk + a, :]
+                        .unsqueeze(1)
+                        .to_broadcast([P, PIX, PACK]),
                         op=ALU.add,
                     )
                 return biased
 
-            def quantise_red(chunk, biased):
-                flipped = psum.tile(
-                    [P, TILES_PER_CHUNK, PACK, PIX], BF16, tag="scratch", bufs=SCRATCH_BANKS
-                )
-                for a in range(TILES_PER_CHUNK):
-                    for t in range(PACK):
-                        nc.tensor.transpose(flipped[:, a, t, :], biased[:, a, t, :], ident_bf16[:])
+            def rectify_red(biased):
                 red_grouped = early.tile([P, TILES_PER_CHUNK, PIX, PACK], BF16, bufs=2, align_bytes=64)
-                nc.scalar.activation(
-                    out=red_grouped[:], in_=flipped[:].rearrange("q a t n -> q a n t"), func=ACT.Relu
-                )
+                nc.vector.tensor_scalar_max(out=red_grouped[:], in0=biased[:], scalar1=0.0)
+                return red_grouped
+
+            def quantise_red(chunk, red_grouped):
                 passes = slice(TILES_PER_CHUNK * chunk, TILES_PER_CHUNK * (chunk + 1))
                 nc.vector.quantize_mx(
                     out=red_codes[:, passes, :].rearrange("q a n -> q (a n)").bitcast(FP8X4),
@@ -266,70 +288,144 @@ def tile_involution_k_kernel(
                     in_=red_grouped[:].rearrange("q a n t -> q (a n t)"),
                 )
 
-            biased_ahead = reduce_product(0)
+            for tap in range(HEAD_TAPS):
+                shift_image(tap)
+            raw_ahead = reduce_product(0)
+            biased_behind = None
             for chunk in range(REDUCE_CHUNKS):
-                biased_now = biased_ahead
+                raw_now = raw_ahead
                 if chunk + 1 < REDUCE_CHUNKS:
-                    biased_ahead = reduce_product(chunk + 1)
-                quantise_red(chunk, biased_now)
+                    raw_ahead = reduce_product(chunk + 1)
+                if chunk > 0:
+                    red_behind = rectify_red(biased_behind)
+                biased_now = flip_red(chunk, raw_now)
+                if chunk > 0:
+                    quantise_red(chunk - 1, red_behind)
+                biased_behind = biased_now
+                shift_image(HEAD_TAPS + chunk)
+            red_behind = rectify_red(biased_behind)
+            quantise_red(REDUCE_CHUNKS - 1, red_behind)
+            for first_row in range(0, SPAN_BIAS_ROWS, ROWS_PER_BANK):
+                spread_span_bias(first_row, min(ROWS_PER_BANK, SPAN_BIAS_ROWS - first_row))
 
         late = ctx.enter_context(tc.tile_pool(name="late", bufs=2))
         products = {}
 
-        def span_product(first_col, width):
-            cols = slice(first_col, first_col + width)
-            acc = psum.tile([P, BANK_F32], F32, tag="acc", bufs=ACC_BANKS)
-            for first_pass in range(0, R_PASSES, PASSES_PER_LOAD):
+        def rest_of_images(load, loads):
+            left = TAPS - HEAD_TAPS - REDUCE_CHUNKS
+            first_tap = TAPS - left
+            for tap in range(first_tap + left * load // loads, first_tap + left * (load + 1) // loads):
+                shift_image(tap)
+
+        def nothing(load, loads):
+            pass
+
+        banks = []
+        block_banks = []
+        for width in SPAN_BLOCKS:
+            numbers = []
+            left = width
+            for mm_width in MM_WIDTHS:
+                while left >= mm_width:
+                    first_col = banks[-1][0] + banks[-1][1] if banks else 0
+                    numbers.append(len(banks))
+                    banks.append((first_col, mm_width))
+                    left -= mm_width
+            block_banks.append(numbers)
+        block_parts = []
+        group = 0
+        for numbers in block_banks:
+            last_col, last_width = banks[numbers[-1]]
+            end_group = (last_col + last_width) // TAPS
+            if end_group < GROUPS - GROUPS_PER_TILE:
+                end_group -= end_group % HALF_TILE
+            parts = []
+            while group < end_group:
+                part_end = min(end_group, PART_GROUPS * (group // PART_GROUPS + 1))
+                parts.append((group, part_end))
+                group = part_end
+            block_parts.append(parts)
+        accs = {}
+        exponentials = {}
+        totals = {}
+        inverses = {}
+        probs = {}
+
+        def add_taps(c_tile):
+            summed = psum.tile([P, PIX], F32, tag="scratch", bufs=SCRATCH_BANKS)
+            for tap in range(TAPS):
+                nc.tensor.matmul(
+                    out=summed[:],
+                    lhsT=products[c_tile][:, tap, :],
+                    rhs=ident_f32[:],
+                    start=(tap == 0),
+                    stop=(tap == TAPS - 1),
+                    is_transpose=True,
+                )
+            return summed
+
+        def store(c_tile, summed):
+            result = late.tile([P, PIX], F32)
+            nc.scalar.copy(out=result[:], in_=summed[:])
+            nc.scalar.dma_start(out=out_rows[P * c_tile : P * (c_tile + 1), :], in_=result[:])
+
+        def span_product(block, ready, between_loads):
+            width = SPAN_BLOCKS[block]
+            first_col = banks[block_banks[block][0]][0]
+            for b in block_banks[block]:
+                accs[b] = psum.tile([P, BANK_F32], F32, tag="acc", bufs=ACC_BANKS, name="acc")
+            passes = MAX_PASSES_PER_LOAD
+            while passes * width > STREAM_WORDS:
+                passes //= 2
+            loads = R_PASSES // passes
+            for load in range(loads):
+                first_pass = passes * load
                 words = stream.tile(
                     [P, STREAM_WORDS], U32, tag="words", name="span_words", align_bytes=64
                 )
                 nc.sync.dma_start(
-                    out=words[:, : PASSES_PER_LOAD * width].rearrange("p (g n) -> p g n", n=width).bitcast(I32),
+                    out=words[:, : passes * width].rearrange("p (g n) -> p g n", n=width).bitcast(I32),
                     in_=span_bytes[
-                        :,
-                        first_pass : first_pass + PASSES_PER_LOAD,
-                        PACK * first_col : PACK * (first_col + width),
+                        :, first_pass : first_pass + passes, PACK * first_col : PACK * (first_col + width)
                     ].bitcast(I32),
                 )
-                for g in range(first_pass, first_pass + PASSES_PER_LOAD):
-                    first_word = width * (g - first_pass)
-                    nc.tensor.matmul_mx(
-                        out=acc[:, :width],
-                        lhsT=red_codes[:, g, :].bitcast(FP8X4),
-                        lhsT_scale=red_scales[:, g, :],
-                        rhs=words[:, first_word : first_word + width].bitcast(FP8X4),
-                        rhs_scale=span_planes[
-                            ROWS_PER_QUADRANT * (g % PLANES_PER_TILE) : P, g // PLANES_PER_TILE, cols
-                        ],
-                        start=(g == 0),
-                        stop=(g == R_PASSES - 1),
-                    )
-            return acc
+                for g in range(first_pass, first_pass + passes):
+                    for b in block_banks[block]:
+                        bank_col, bank_width = banks[b]
+                        first_word = width * (g - first_pass) + bank_col - first_col
+                        nc.tensor.matmul_mx(
+                            out=accs[b][:, :bank_width],
+                            lhsT=red_codes[:, g, :].bitcast(FP8X4),
+                            lhsT_scale=red_scales[:, g, :],
+                            rhs=words[:, first_word : first_word + bank_width].bitcast(FP8X4),
+                            rhs_scale=span_planes[
+                                ROWS_PER_QUADRANT * (g % PLANES_PER_TILE) : P,
+                                g // PLANES_PER_TILE,
+                                bank_col : bank_col + bank_width,
+                            ],
+                            start=(g == 0),
+                            stop=(g == R_PASSES - 1),
+                        )
+                between_loads(load, loads)
+            return [(c_tile, add_taps(c_tile)) for c_tile in ready]
 
-        n_blocks = len(SPAN_BLOCKS)
-        block_starts = [sum(SPAN_BLOCKS[:b]) for b in range(n_blocks)]
-        end_groups = [(block_starts[b] + SPAN_BLOCKS[b]) // TAPS for b in range(n_blocks)]
-        first_groups = [0] + end_groups[:-1]
-        accs = {}
-        exponentials = {}
-        totals = {}
-        finished = {}
-        sums = {}
-
-        def exponentiate(b):
-            cols = slice(block_starts[b], block_starts[b] + SPAN_BLOCKS[b])
+        def add_bias(b):
+            first_col, width = banks[b]
+            cols = slice(first_col, first_col + width)
             nc.vector.tensor_tensor(
-                out=kern[:, cols], in0=accs[b][:, : SPAN_BLOCKS[b]], in1=span_bias[:, cols], op=ALU.add
+                out=kern[:, cols], in0=accs[b][:, :width], in1=span_bias[:, cols], op=ALU.add
             )
-            n = end_groups[b] - first_groups[b]
-            logits = kern[:, TAPS * first_groups[b] : TAPS * end_groups[b]].rearrange(
-                "p (g t) -> p g t", t=TAPS
+
+        def exponentiate(part):
+            first, end = part
+            logits = kern[:, TAPS * first : TAPS * end].rearrange("p (g t) -> p g t", t=TAPS)
+            minus_top = late.tile([P, PART_GROUPS], F32, bufs=PART_BUFS)
+            nc.vector.tensor_reduce(
+                out=minus_top[:, : end - first], in_=logits, axis=AXIS_X, op=ALU.max, negate=True
             )
-            minus_top = late.tile([P, MAX_GROUPS], F32)
-            nc.vector.tensor_reduce(out=minus_top[:, :n], in_=logits, axis=AXIS_X, op=ALU.max, negate=True)
-            expd = late.tile([P, MAX_GROUPS, TAPS], F32)
-            total = late.tile([P, MAX_GROUPS], F32)
-            for g in range(n):
+            expd = late.tile([P, PART_GROUPS, TAPS], F32, bufs=PART_BUFS)
+            total = late.tile([P, PART_GROUPS], F32, bufs=PART_BUFS)
+            for g in range(end - first):
                 nc.scalar.activation(
                     out=expd[:, g, :],
                     in_=logits[:, g, :],
@@ -337,74 +433,68 @@ def tile_involution_k_kernel(
                     bias=minus_top[:, g : g + 1],
                     accum_out=total[:, g : g + 1],
                 )
-            exponentials[b] = expd
-            totals[b] = total
+            exponentials[part] = expd
+            totals[part] = total
 
-        def multiply(b):
-            n = end_groups[b] - first_groups[b]
-            expd = exponentials[b]
-            inverse = late.tile([P, MAX_GROUPS], F32)
-            nc.vector.reciprocal(out=inverse[:, :n], in_=totals[b][:, :n])
-            prob = late.tile([P, MAX_GROUPS, TAPS], F32)
+        def invert(part):
+            n = part[1] - part[0]
+            inverse = late.tile([P, PART_GROUPS], F32)
+            nc.vector.reciprocal(out=inverse[:, :n], in_=totals[part][:, :n])
+            inverses[part] = inverse
+
+        def normalise(part):
+            n = part[1] - part[0]
+            prob = late.tile([P, PART_GROUPS, TAPS], F32)
             nc.vector.tensor_tensor(
                 out=prob[:, :n, :],
-                in0=expd[:, :n, :],
-                in1=inverse[:, :n].unsqueeze(2).to_broadcast([P, n, TAPS]),
+                in0=exponentials[part][:, :n, :],
+                in1=inverses[part][:, :n].unsqueeze(2).to_broadcast([P, n, TAPS]),
                 op=ALU.mult,
             )
-            finished[b] = []
-            group = first_groups[b]
-            while group < end_groups[b]:
-                c_tile = group // GROUPS_PER_TILE
-                piece_end = min(end_groups[b], GROUPS_PER_TILE * (c_tile + 1))
-                if group == GROUPS_PER_TILE * c_tile:
-                    products[c_tile] = late.tile([P, TAPS, P], F32, name="products", bufs=PRODUCT_BUFS)
-                piece = products[c_tile][
-                    :, :, CH_PER_GROUP * group - P * c_tile : CH_PER_GROUP * piece_end - P * c_tile
-                ]
-                nc.vector.tensor_tensor(
-                    out=piece.rearrange("p t (g c) -> p t g c", c=CH_PER_GROUP),
-                    in0=shifted[:, :, CH_PER_GROUP * group : CH_PER_GROUP * piece_end].rearrange(
-                        "p t (g c) -> p t g c", c=CH_PER_GROUP
-                    ),
-                    in1=prob[:, group - first_groups[b] : piece_end - first_groups[b], :]
-                    .rearrange("p g t -> p t g")
-                    .unsqueeze(3)
-                    .to_broadcast([P, TAPS, piece_end - group, CH_PER_GROUP]),
-                    op=ALU.mult,
-                )
-                group = piece_end
-                if group == GROUPS_PER_TILE * (c_tile + 1):
-                    finished[b].append(c_tile)
+            probs[part] = prob
 
-        def add_taps(b):
-            sums[b] = []
-            for c_tile in finished[b]:
-                summed = psum.tile([P, PIX], F32, tag="scratch", bufs=SCRATCH_BANKS)
-                for tap in range(TAPS):
-                    nc.tensor.matmul(
-                        out=summed[:],
-                        lhsT=products[c_tile][:, tap, :],
-                        rhs=ident_f32[:],
-                        start=(tap == 0),
-                        stop=(tap == TAPS - 1),
-                        is_transpose=True,
-                    )
-                sums[b].append((c_tile, summed))
+        def multiply(part):
+            first, end = part
+            n = end - first
+            c_tile = first // GROUPS_PER_TILE
+            if first == GROUPS_PER_TILE * c_tile:
+                products[c_tile] = late.tile([P, TAPS, P], F32, name="products", bufs=PRODUCT_BUFS)
+            piece = products[c_tile][:, :, CH_PER_GROUP * first - P * c_tile : CH_PER_GROUP * end - P * c_tile]
+            nc.vector.tensor_tensor(
+                out=piece.rearrange("p t (g c) -> p t g c", c=CH_PER_GROUP),
+                in0=shifted[:, :, CH_PER_GROUP * first : CH_PER_GROUP * end].rearrange(
+                    "p t (g c) -> p t g c", c=CH_PER_GROUP
+                ),
+                in1=probs[part][:, :n, :]
+                .rearrange("p g t -> p t g")
+                .unsqueeze(3)
+                .to_broadcast([P, TAPS, n, CH_PER_GROUP]),
+                op=ALU.mult,
+            )
+            return [c_tile] if end == GROUPS_PER_TILE * (c_tile + 1) else []
 
-        def store(b):
-            for c_tile, summed in sums[b]:
-                result = late.tile([P, PIX], F32)
-                nc.scalar.copy(out=result[:], in_=summed[:])
-                nc.scalar.dma_start(out=out_rows[P * c_tile : P * (c_tile + 1), :], in_=result[:])
-
-        for step in range(n_blocks + 3):
-            if step < n_blocks:
-                accs[step] = span_product(block_starts[step], SPAN_BLOCKS[step])
-            if 0 <= step - 1 < n_blocks:
-                exponentiate(step - 1)
-            if 0 <= step - 2 < n_blocks:
-                multiply(step - 2)
-                add_taps(step - 2)
-            if 0 <= step - 3 < n_blocks:
-                store(step - 3)
+        ready = []
+        waiting = None
+        for block in range(len(SPAN_BLOCKS)):
+            sums = span_product(block, ready, rest_of_images if block == 0 else nothing)
+            for b in block_banks[block]:
+                add_bias(b)
+            ready = []
+            parts = block_parts[block]
+            for i, part in enumerate(parts):
+                exponentiate(part)
+            for c_tile, summed in sums:
+                store(c_tile, summed)
+            if waiting:
+                ready += multiply(waiting)
+            invert(parts[0])
+            for i, part in enumerate(parts):
+                if i + 1 < len(parts):
+                    invert(parts[i + 1])
+                normalise(part)
+                if i > 0:
+                    ready += multiply(parts[i - 1])
+            waiting = parts[-1]
+        ready += multiply(waiting)
+        for c_tile in ready:
+            store(c_tile, add_taps(c_tile))

@@ -39,7 +39,8 @@ GROUPS_PER_TILE = P // CH_PER_GROUP
 
 STREAM_WORDS = 2048
 STREAM_BUFS = 8
-REDUCE_CHUNK = STREAM_WORDS // C_PASSES
+REDUCE_UNITS = R // STREAM_WORDS
+REDUCE_CHUNK = 1024
 REDUCE_CHUNKS = R // REDUCE_CHUNK
 TILES_PER_CHUNK = REDUCE_CHUNK // BANK_F32
 
@@ -53,7 +54,7 @@ PART_BUFS = 3
 PLANES_PER_TILE = 4
 QUADRANTS = 4
 ROWS_PER_QUADRANT = 4
-REDUCE_PLANE_COLS = R * C_PASSES // PLANES_PER_TILE
+REDUCE_PLANE_COLS = R // PLANES_PER_TILE
 
 SPAN_BIAS_ROWS = O // P
 ROWS_PER_BANK = BANK_BF16 // P
@@ -95,7 +96,7 @@ def tile_involution_k_kernel(
         with tc.tile_pool(name="early", bufs=1) as early:
             x_scales = early.tile([P, C_PASSES, PIX], U8, align_bytes=64)
             x_codes = early.tile([P, C_PASSES, PIX], U32, align_bytes=64)
-            reduce_planes = early.tile([P, REDUCE_PLANE_COLS], U8, align_bytes=64)
+            reduce_planes = early.tile([P, C_PASSES, REDUCE_PLANE_COLS], U8, align_bytes=64)
             make_identity(nc, ident_f32[:])
             make_identity(nc, ident_bf16[:])
 
@@ -103,7 +104,7 @@ def tile_involution_k_kernel(
             span_bias_rows = early.tile([P, P], BF16)
             nc.vector.memset(reduce_bias_rows[:], 0.0)
             nc.vector.memset(span_bias_rows[:], 0.0)
-            nc.vector.memset(reduce_planes[:].bitcast(I32), 0)
+            nc.vector.memset(reduce_planes[:].rearrange("p g n -> p (g n)").bitcast(I32), 0)
 
             x_by_word = early.tile([P, C_PASSES, PACK, PIX], BF16)
             nc.scalar.dma_start(
@@ -116,29 +117,32 @@ def tile_involution_k_kernel(
                 out=span_bias_rows[0:SPAN_BIAS_ROWS, :], in_=b_span.rearrange("(m n) -> m n", n=P)
             )
 
-            for quadrant in range(QUADRANTS):
-                for half in range(2):
-                    first_row = 32 * quadrant + 8 * half
+            reduce_words = []
+            for unit in range(REDUCE_UNITS):
+                unit_words = []
+                for g in range(C_PASSES):
+                    words = stream.tile(
+                        [P, STREAM_WORDS], U32, tag="words", name="reduce_words", align_bytes=64
+                    )
                     nc.sync.dma_start(
-                        out=reduce_planes[first_row : first_row + 8, :].bitcast(I32),
-                        in_=w_reduce_scales[
-                            :,
-                            ROWS_PER_QUADRANT * quadrant : ROWS_PER_QUADRANT * (quadrant + 1),
-                            REDUCE_PLANE_COLS * half : REDUCE_PLANE_COLS * (half + 1),
+                        out=words[:].bitcast(I32),
+                        in_=reduce_bytes[
+                            :, g, PACK * STREAM_WORDS * unit : PACK * STREAM_WORDS * (unit + 1)
                         ].bitcast(I32),
                     )
-            reduce_words = []
-            for chunk in range(REDUCE_CHUNKS):
-                words = stream.tile(
-                    [P, STREAM_WORDS], U32, tag="words", name="reduce_words", align_bytes=64
-                )
-                nc.sync.dma_start(
-                    out=words[:].rearrange("p (g n) -> p g n", g=C_PASSES).bitcast(I32),
-                    in_=reduce_bytes[
-                        :, :, PACK * REDUCE_CHUNK * chunk : PACK * REDUCE_CHUNK * (chunk + 1)
-                    ].bitcast(I32),
-                )
-                reduce_words.append(words)
+                    unit_words.append(words)
+                reduce_words.append(unit_words)
+                if unit == 0:
+                    for g in range(C_PASSES):
+                        for quadrant in range(QUADRANTS):
+                            nc.sync.dma_start(
+                                out=reduce_planes[32 * quadrant : 32 * quadrant + 16, g, :].bitcast(I32),
+                                in_=w_reduce_scales[
+                                    g, ROWS_PER_QUADRANT * quadrant : ROWS_PER_QUADRANT * (quadrant + 1), :
+                                ]
+                                .bitcast(I32)
+                                .rearrange("q (j n) -> j q n", j=PLANES_PER_TILE),
+                            )
 
             nc.gpsimd.memset(span_planes[:].rearrange("p a n -> p (a n)").bitcast(F32), 0.0)
 
@@ -236,17 +240,17 @@ def tile_involution_k_kernel(
                 raw = early.tile([P, TILES_PER_CHUNK, BANK_F32], F32, bufs=2)
                 for a in range(TILES_PER_CHUNK):
                     first_r = REDUCE_CHUNK * chunk + BANK_F32 * a
-                    half, plane_col = divmod(first_r, REDUCE_PLANE_COLS)
+                    unit, unit_col = divmod(first_r, STREAM_WORDS)
+                    quarter, plane_col = divmod(first_r, REDUCE_PLANE_COLS)
                     acc = psum.tile([P, BANK_F32], F32, tag="acc", bufs=ACC_BANKS)
                     for g in range(C_PASSES):
-                        first_word = REDUCE_CHUNK * g + BANK_F32 * a
                         nc.tensor.matmul_mx(
                             out=acc[:],
                             lhsT=x_codes[:, g, :].bitcast(FP8X4),
                             lhsT_scale=x_scales[:, g, :],
-                            rhs=reduce_words[chunk][:, first_word : first_word + BANK_F32].bitcast(FP8X4),
+                            rhs=reduce_words[unit][g][:, unit_col : unit_col + BANK_F32].bitcast(FP8X4),
                             rhs_scale=reduce_planes[
-                                ROWS_PER_QUADRANT * (2 * half + g) : P, plane_col : plane_col + BANK_F32
+                                ROWS_PER_QUADRANT * quarter : P, g, plane_col : plane_col + BANK_F32
                             ],
                             start=(g == 0),
                             stop=(g == C_PASSES - 1),

@@ -44,7 +44,7 @@ REDUCE_CHUNK = 1024
 REDUCE_CHUNKS = R // REDUCE_CHUNK
 TILES_PER_CHUNK = REDUCE_CHUNK // BANK_F32
 
-SPAN_BLOCKS = [512, 640, 768, 512, 384, 256, 128]
+SPAN_BLOCKS = [1024, 768, 640, 384, 256, 128]
 MM_WIDTHS = [512, 256, 128]
 MAX_PASSES_PER_LOAD = 8
 PART_GROUPS = 16
@@ -144,8 +144,6 @@ def tile_involution_k_kernel(
                                 .rearrange("q (j n) -> j q n", j=PLANES_PER_TILE),
                             )
 
-            nc.gpsimd.memset(span_planes[:].rearrange("p a n -> p (a n)").bitcast(F32), 0.0)
-
             x_masked = keep.tile([P, K, PAIR_TILES, FLAT], F32)
             nc.vector.memset(x_masked[:, :, :, 0:FLAT_PAD], 0.0)
             nc.vector.memset(x_masked[:, :, :, FLAT_PAD + PIX : FLAT], 0.0)
@@ -225,6 +223,7 @@ def tile_involution_k_kernel(
                     in_=window[:].rearrange("n g u p -> n g p u"),
                 )
 
+            nc.vector.memset(span_planes[:].rearrange("p a n -> p (a n)").bitcast(I32), 0)
             for slab in range(R_PASSES // PLANES_PER_TILE):
                 for quadrant in range(QUADRANTS):
                     nc.sync.dma_start(
@@ -457,40 +456,35 @@ def tile_involution_k_kernel(
             )
             probs[part] = prob
 
-        def multiply(part):
+        def multiply(part, cuts=(0, TAPS)):
             first, end = part
             n = end - first
             c_tile = first // GROUPS_PER_TILE
             if first == GROUPS_PER_TILE * c_tile:
                 products[c_tile] = late.tile([P, TAPS, P], F32, name="products", bufs=PRODUCT_BUFS)
             piece = products[c_tile][:, :, CH_PER_GROUP * first - P * c_tile : CH_PER_GROUP * end - P * c_tile]
-            nc.vector.tensor_tensor(
-                out=piece.rearrange("p t (g c) -> p t g c", c=CH_PER_GROUP),
-                in0=shifted[:, :, CH_PER_GROUP * first : CH_PER_GROUP * end].rearrange(
-                    "p t (g c) -> p t g c", c=CH_PER_GROUP
-                ),
-                in1=probs[part][:, :n, :]
-                .rearrange("p g t -> p t g")
-                .unsqueeze(3)
-                .to_broadcast([P, TAPS, n, CH_PER_GROUP]),
-                op=ALU.mult,
-            )
+            images = shifted[:, :, CH_PER_GROUP * first : CH_PER_GROUP * end]
+            by_tap = probs[part][:, :n, :].rearrange("p g t -> p t g")
+            for lo, hi in zip(cuts, cuts[1:]):
+                nc.vector.tensor_tensor(
+                    out=piece[:, lo:hi, :].rearrange("p t (g c) -> p t g c", c=CH_PER_GROUP),
+                    in0=images[:, lo:hi, :].rearrange("p t (g c) -> p t g c", c=CH_PER_GROUP),
+                    in1=by_tap[:, lo:hi, :].unsqueeze(3).to_broadcast([P, hi - lo, n, CH_PER_GROUP]),
+                    op=ALU.mult,
+                )
             return [c_tile] if end == GROUPS_PER_TILE * (c_tile + 1) else []
 
         ready = []
-        waiting = None
         for block in range(len(SPAN_BLOCKS)):
             sums = span_product(block, ready, rest_of_images if block == 0 else nothing)
             for b in block_banks[block]:
                 add_bias(b)
             ready = []
             parts = block_parts[block]
-            for i, part in enumerate(parts):
+            for part in parts:
                 exponentiate(part)
             for c_tile, summed in sums:
                 store(c_tile, summed)
-            if waiting:
-                ready += multiply(waiting)
             invert(parts[0])
             for i, part in enumerate(parts):
                 if i + 1 < len(parts):
@@ -498,7 +492,7 @@ def tile_involution_k_kernel(
                 normalise(part)
                 if i > 0:
                     ready += multiply(parts[i - 1])
-            waiting = parts[-1]
-        ready += multiply(waiting)
+            is_last = block == len(SPAN_BLOCKS) - 1
+            ready += multiply(parts[-1], (0, TAPS // 2, TAPS) if is_last else (0, TAPS))
         for c_tile in ready:
             store(c_tile, add_taps(c_tile))

@@ -36,6 +36,7 @@ C_TILES = C // P
 PAIRS = PACK // 2
 PAIR_TILES = C_PASSES * PAIRS
 GROUPS_PER_TILE = P // CH_PER_GROUP
+MAX_READY = BANK_F32 // PIX
 
 STREAM_WORDS = 2048
 STREAM_BUFS = 8
@@ -44,12 +45,13 @@ REDUCE_CHUNK = 1024
 REDUCE_CHUNKS = R // REDUCE_CHUNK
 TILES_PER_CHUNK = REDUCE_CHUNK // BANK_F32
 
-SPAN_BLOCKS = [1024, 768, 640, 384, 256, 128]
+SPAN_BLOCKS = [512, 896, 896, 512, 256, 128]
 MM_WIDTHS = [512, 256, 128]
 MAX_PASSES_PER_LOAD = 8
+LAST_PASSES = 2
 PART_GROUPS = 16
 HALF_TILE = PART_GROUPS // 2
-PART_BUFS = 3
+PART_BUFS = 4
 
 PLANES_PER_TILE = 4
 QUADRANTS = 4
@@ -144,6 +146,9 @@ def tile_involution_k_kernel(
                                 .rearrange("q (j n) -> j q n", j=PLANES_PER_TILE),
                             )
 
+            for slab in range(R_PASSES // PLANES_PER_TILE):
+                nc.gpsimd.memset(span_planes[:, slab, :].bitcast(F32), 0.0)
+
             x_masked = keep.tile([P, K, PAIR_TILES, FLAT], F32)
             nc.vector.memset(x_masked[:, :, :, 0:FLAT_PAD], 0.0)
             nc.vector.memset(x_masked[:, :, :, FLAT_PAD + PIX : FLAT], 0.0)
@@ -207,7 +212,7 @@ def tile_involution_k_kernel(
                     out=span_bias[:, P * first_row : P * (first_row + rows)], in_=bank[:, : P * rows]
                 )
 
-            def shift_image(tap):
+            def shift_image(tap, by_scalar):
                 i, j = divmod(tap, K)
                 first = FLAT_PAD + (i - PAD) * W + (j - PAD)
                 window = psum.tile([P, C_PASSES, PAIRS, P], F32, tag="scratch", bufs=SCRATCH_BANKS)
@@ -217,13 +222,12 @@ def tile_involution_k_kernel(
                         x_masked[:, j, pt, first : first + PIX],
                         ident_f32[:],
                     )
-                copy_out = nc.scalar.copy if tap % 2 == 0 else nc.vector.tensor_copy
+                copy_out = nc.scalar.copy if by_scalar else nc.vector.tensor_copy
                 copy_out(
                     out=shifted[:, tap, :].bitcast(F32).rearrange("n (g p u) -> n g p u", g=C_PASSES, u=PAIRS),
                     in_=window[:].rearrange("n g u p -> n g p u"),
                 )
 
-            nc.vector.memset(span_planes[:].rearrange("p a n -> p (a n)").bitcast(I32), 0)
             for slab in range(R_PASSES // PLANES_PER_TILE):
                 for quadrant in range(QUADRANTS):
                     nc.sync.dma_start(
@@ -292,7 +296,7 @@ def tile_involution_k_kernel(
                 )
 
             for tap in range(HEAD_TAPS):
-                shift_image(tap)
+                shift_image(tap, tap % 2 == 0)
             raw_ahead = reduce_product(0)
             biased_behind = None
             for chunk in range(REDUCE_CHUNKS):
@@ -305,7 +309,7 @@ def tile_involution_k_kernel(
                 if chunk > 0:
                     quantise_red(chunk - 1, red_behind)
                 biased_behind = biased_now
-                shift_image(HEAD_TAPS + chunk)
+                shift_image(HEAD_TAPS + chunk, True)
             red_behind = rectify_red(biased_behind)
             quantise_red(REDUCE_CHUNKS - 1, red_behind)
             for first_row in range(0, SPAN_BIAS_ROWS, ROWS_PER_BANK):
@@ -318,7 +322,7 @@ def tile_involution_k_kernel(
             left = TAPS - HEAD_TAPS - REDUCE_CHUNKS
             first_tap = TAPS - left
             for tap in range(first_tap + left * load // loads, first_tap + left * (load + 1) // loads):
-                shift_image(tap)
+                shift_image(tap, tap % 2 == 0)
 
         def nothing(load, loads):
             pass
@@ -351,8 +355,8 @@ def tile_involution_k_kernel(
         accs = {}
         exponentials = {}
         totals = {}
+        group_inverses = {}
         inverses = {}
-        probs = {}
 
         def add_taps(c_tile):
             summed = psum.tile([P, PIX], F32, tag="scratch", bufs=SCRATCH_BANKS)
@@ -367,9 +371,23 @@ def tile_involution_k_kernel(
                 )
             return summed
 
-        def store(c_tile, summed):
-            result = late.tile([P, PIX], F32)
-            nc.scalar.copy(out=result[:], in_=summed[:])
+        def flip_inverses(c_tiles):
+            flipped = psum.tile([P, MAX_READY, PIX], F32, tag="scratch", bufs=SCRATCH_BANKS)
+            for i, c_tile in enumerate(c_tiles):
+                nc.tensor.transpose(flipped[:, i, :], inverses[c_tile][:], ident_f32[:])
+            return flipped
+
+        def copy_inverses(n, flipped):
+            rows = late.tile([P, MAX_READY, PIX], F32)
+            nc.scalar.copy(out=rows[:, :n, :], in_=flipped[:, :n, :])
+            return rows
+
+        def scale_sum(summed, inverse):
+            result = late.tile([P, PIX], F32, bufs=PRODUCT_BUFS)
+            nc.vector.tensor_tensor(out=result[:], in0=summed[:], in1=inverse, op=ALU.mult)
+            return result
+
+        def store(c_tile, result):
             nc.scalar.dma_start(out=out_rows[P * c_tile : P * (c_tile + 1), :], in_=result[:])
 
         def span_product(block, ready, between_loads):
@@ -380,9 +398,12 @@ def tile_involution_k_kernel(
             passes = MAX_PASSES_PER_LOAD
             while passes * width > STREAM_WORDS:
                 passes //= 2
-            loads = R_PASSES // passes
-            for load in range(loads):
-                first_pass = passes * load
+            load_passes = [passes] * (R_PASSES // passes)
+            if block == len(SPAN_BLOCKS) - 1:
+                load_passes[-1:] = [passes - LAST_PASSES, LAST_PASSES]
+            loads = len(load_passes)
+            for load, passes in enumerate(load_passes):
+                first_pass = sum(load_passes[:load])
                 words = stream.tile(
                     [P, STREAM_WORDS], U32, tag="words", name="span_words", align_bytes=64
                 )
@@ -410,7 +431,8 @@ def tile_involution_k_kernel(
                             stop=(g == R_PASSES - 1),
                         )
                 between_loads(load, loads)
-            return [(c_tile, add_taps(c_tile)) for c_tile in ready]
+            flipped = flip_inverses(ready) if ready else None
+            return flipped, [add_taps(c_tile) for c_tile in ready]
 
         def add_bias(b):
             first_col, width = banks[b]
@@ -440,21 +462,26 @@ def tile_involution_k_kernel(
             totals[part] = total
 
         def invert(part):
-            n = part[1] - part[0]
-            inverse = late.tile([P, PART_GROUPS], F32)
-            nc.vector.reciprocal(out=inverse[:, :n], in_=totals[part][:, :n])
-            inverses[part] = inverse
+            first, end = part
+            n = end - first
+            c_tile = first // GROUPS_PER_TILE
+            if first == GROUPS_PER_TILE * c_tile:
+                inverses[c_tile] = late.tile([P, P], F32, name="inverses", bufs=PRODUCT_BUFS)
+            group_inverse = late.tile([P, PART_GROUPS], F32, bufs=PART_BUFS)
+            nc.vector.reciprocal(out=group_inverse[:, :n], in_=totals[part][:, :n])
+            group_inverses[part] = group_inverse
 
-        def normalise(part):
-            n = part[1] - part[0]
-            prob = late.tile([P, PART_GROUPS, TAPS], F32)
-            nc.vector.tensor_tensor(
-                out=prob[:, :n, :],
-                in0=exponentials[part][:, :n, :],
-                in1=inverses[part][:, :n].unsqueeze(2).to_broadcast([P, n, TAPS]),
-                op=ALU.mult,
+        def spread_inverse(part):
+            first, end = part
+            n = end - first
+            c_tile = first // GROUPS_PER_TILE
+            nc.scalar.activation(
+                out=inverses[c_tile][
+                    :, CH_PER_GROUP * first - P * c_tile : CH_PER_GROUP * end - P * c_tile
+                ].rearrange("p (g c) -> p g c", c=CH_PER_GROUP),
+                in_=group_inverses[part][:, :n].unsqueeze(2).to_broadcast([P, n, CH_PER_GROUP]),
+                func=ACT.Copy,
             )
-            probs[part] = prob
 
         def multiply(part, cuts=(0, TAPS)):
             first, end = part
@@ -464,7 +491,7 @@ def tile_involution_k_kernel(
                 products[c_tile] = late.tile([P, TAPS, P], F32, name="products", bufs=PRODUCT_BUFS)
             piece = products[c_tile][:, :, CH_PER_GROUP * first - P * c_tile : CH_PER_GROUP * end - P * c_tile]
             images = shifted[:, :, CH_PER_GROUP * first : CH_PER_GROUP * end]
-            by_tap = probs[part][:, :n, :].rearrange("p g t -> p t g")
+            by_tap = exponentials[part][:, :n, :].rearrange("p g t -> p t g")
             for lo, hi in zip(cuts, cuts[1:]):
                 nc.vector.tensor_tensor(
                     out=piece[:, lo:hi, :].rearrange("p t (g c) -> p t g c", c=CH_PER_GROUP),
@@ -475,24 +502,29 @@ def tile_involution_k_kernel(
             return [c_tile] if end == GROUPS_PER_TILE * (c_tile + 1) else []
 
         ready = []
+        waiting = None
         for block in range(len(SPAN_BLOCKS)):
-            sums = span_product(block, ready, rest_of_images if block == 0 else nothing)
+            flipped, sums = span_product(block, ready, rest_of_images if block == 0 else nothing)
             for b in block_banks[block]:
                 add_bias(b)
-            ready = []
             parts = block_parts[block]
             for part in parts:
                 exponentiate(part)
-            for c_tile, summed in sums:
-                store(c_tile, summed)
-            invert(parts[0])
-            for i, part in enumerate(parts):
-                if i + 1 < len(parts):
-                    invert(parts[i + 1])
-                normalise(part)
-                if i > 0:
-                    ready += multiply(parts[i - 1])
-            is_last = block == len(SPAN_BLOCKS) - 1
-            ready += multiply(parts[-1], (0, TAPS // 2, TAPS) if is_last else (0, TAPS))
-        for c_tile in ready:
-            store(c_tile, add_taps(c_tile))
+            inverse_rows = copy_inverses(len(ready), flipped) if ready else None
+            summed_tiles = ready
+            ready = []
+            if waiting:
+                ready += multiply(waiting)
+            for part in parts:
+                invert(part)
+                spread_inverse(part)
+                if part != parts[-1]:
+                    ready += multiply(part)
+            for i, c_tile in enumerate(summed_tiles):
+                store(c_tile, scale_sum(sums[i], inverse_rows[:, i, :]))
+            waiting = parts[-1]
+        ready += multiply(waiting, (0, TAPS // 2, TAPS))
+        flipped = flip_inverses(ready)
+        inverse_rows = copy_inverses(len(ready), flipped)
+        for i, c_tile in enumerate(ready):
+            store(c_tile, scale_sum(add_taps(c_tile), inverse_rows[:, i, :]))

@@ -45,11 +45,12 @@ REDUCE_CHUNK = 1024
 REDUCE_CHUNKS = R // REDUCE_CHUNK
 TILES_PER_CHUNK = REDUCE_CHUNK // BANK_F32
 
-SPAN_BLOCKS = [512, 896, 896, 512, 256, 128]
+SPAN_BLOCKS = [640, 1024, 768, 384, 256, 128]
 MM_WIDTHS = [512, 256, 128]
 MAX_PASSES_PER_LOAD = 8
 LAST_PASSES = 2
 PART_GROUPS = 16
+LAST_TILE_GROUPS = 6
 HALF_TILE = PART_GROUPS // 2
 PART_BUFS = 4
 
@@ -96,6 +97,11 @@ def tile_involution_k_kernel(
         kern = keep.tile([P, O], F32)
 
         with tc.tile_pool(name="early", bufs=1) as early:
+            one = early.tile([P, 1], F32)
+            nc.vector.memset(one[:], 1.0)
+            exp_of_one = early.tile([P, 1], F32)
+            nc.scalar.activation(out=exp_of_one[:], in_=one[:], func=ACT.Exp)
+
             x_scales = early.tile([P, C_PASSES, PIX], U8, align_bytes=64)
             x_codes = early.tile([P, C_PASSES, PIX], U32, align_bytes=64)
             reduce_planes = early.tile([P, C_PASSES, REDUCE_PLANE_COLS], U8, align_bytes=64)
@@ -349,6 +355,8 @@ def tile_involution_k_kernel(
             parts = []
             while group < end_group:
                 part_end = min(end_group, PART_GROUPS * (group // PART_GROUPS + 1))
+                if group >= GROUPS - GROUPS_PER_TILE:
+                    part_end = min(part_end, group + LAST_TILE_GROUPS)
                 parts.append((group, part_end))
                 group = part_end
             block_parts.append(parts)
@@ -475,12 +483,11 @@ def tile_involution_k_kernel(
             first, end = part
             n = end - first
             c_tile = first // GROUPS_PER_TILE
-            nc.scalar.activation(
+            nc.scalar.copy(
                 out=inverses[c_tile][
                     :, CH_PER_GROUP * first - P * c_tile : CH_PER_GROUP * end - P * c_tile
                 ].rearrange("p (g c) -> p g c", c=CH_PER_GROUP),
                 in_=group_inverses[part][:, :n].unsqueeze(2).to_broadcast([P, n, CH_PER_GROUP]),
-                func=ACT.Copy,
             )
 
         def multiply(part, cuts=(0, TAPS)):
@@ -503,6 +510,7 @@ def tile_involution_k_kernel(
 
         ready = []
         waiting = None
+        last_block = len(SPAN_BLOCKS) - 1
         for block in range(len(SPAN_BLOCKS)):
             flipped, sums = span_product(block, ready, rest_of_images if block == 0 else nothing)
             for b in block_banks[block]:
@@ -520,10 +528,11 @@ def tile_involution_k_kernel(
                 spread_inverse(part)
                 if part != parts[-1]:
                     ready += multiply(part)
+                elif block == last_block:
+                    ready += multiply(part, (0, TAPS // 2, TAPS))
             for i, c_tile in enumerate(summed_tiles):
                 store(c_tile, scale_sum(sums[i], inverse_rows[:, i, :]))
             waiting = parts[-1]
-        ready += multiply(waiting, (0, TAPS // 2, TAPS))
         flipped = flip_inverses(ready)
         inverse_rows = copy_inverses(len(ready), flipped)
         for i, c_tile in enumerate(ready):

@@ -27,6 +27,7 @@ CH_PER_GROUP = C // GROUPS
 K = 5
 PAD = K // 2
 TAPS = K * K
+CHUNK_TAPS = 2
 HEAD_TAPS = 8
 O = GROUPS * TAPS
 
@@ -97,6 +98,10 @@ def tile_involution_k_kernel(
         kern = keep.tile([P, O], F32)
 
         with tc.tile_pool(name="early", bufs=1) as early:
+            x_by_word = early.tile([P, C_PASSES, PACK, PIX], BF16)
+            nc.scalar.dma_start(
+                out=x_by_word[:], in_=image.rearrange("(g p t) h w -> p g t (h w)", p=P, t=PACK)
+            )
             one = early.tile([P, 1], F32)
             nc.vector.memset(one[:], 1.0)
             exp_of_one = early.tile([P, 1], F32)
@@ -105,25 +110,45 @@ def tile_involution_k_kernel(
             x_scales = early.tile([P, C_PASSES, PIX], U8, align_bytes=64)
             x_codes = early.tile([P, C_PASSES, PIX], U32, align_bytes=64)
             reduce_planes = early.tile([P, C_PASSES, REDUCE_PLANE_COLS], U8, align_bytes=64)
+            nc.vector.memset(reduce_planes[:].rearrange("p g n -> p (g n)").bitcast(I32), 0)
+            reduce_bias_rows = early.tile([P, K_PASS], BF16)
+            span_bias_rows = early.tile([P, P], BF16)
+            nc.gpsimd.memset(reduce_bias_rows[:], 0.0)
+            nc.gpsimd.memset(span_bias_rows[:], 0.0)
+            nc.gpsimd.dma_start(
+                out=reduce_bias_rows[0:R_PASSES, :], in_=b_reduce.rearrange("(m n) -> m n", n=K_PASS)
+            )
+            nc.gpsimd.dma_start(
+                out=span_bias_rows[0:SPAN_BIAS_ROWS, :], in_=b_span.rearrange("(m n) -> m n", n=P)
+            )
             make_identity(nc, ident_f32[:])
             make_identity(nc, ident_bf16[:])
 
-            reduce_bias_rows = early.tile([P, K_PASS], BF16)
-            span_bias_rows = early.tile([P, P], BF16)
-            nc.vector.memset(reduce_bias_rows[:], 0.0)
-            nc.vector.memset(span_bias_rows[:], 0.0)
-            nc.vector.memset(reduce_planes[:].rearrange("p g n -> p (g n)").bitcast(I32), 0)
+            for slab in range(R_PASSES // PLANES_PER_TILE):
+                nc.gpsimd.memset(span_planes[:, slab, :].bitcast(F32), 0.0)
 
-            x_by_word = early.tile([P, C_PASSES, PACK, PIX], BF16)
-            nc.scalar.dma_start(
-                out=x_by_word[:], in_=image.rearrange("(g p t) h w -> p g t (h w)", p=P, t=PACK)
-            )
-            nc.scalar.dma_start(
-                out=reduce_bias_rows[0:R_PASSES, :], in_=b_reduce.rearrange("(m n) -> m n", n=K_PASS)
-            )
-            nc.scalar.dma_start(
-                out=span_bias_rows[0:SPAN_BIAS_ROWS, :], in_=b_span.rearrange("(m n) -> m n", n=P)
-            )
+            def load_reduce_planes():
+                for g in range(C_PASSES):
+                    for quadrant in range(QUADRANTS):
+                        nc.sync.dma_start(
+                            out=reduce_planes[32 * quadrant : 32 * quadrant + 16, g, :].bitcast(I32),
+                            in_=w_reduce_scales[
+                                g, ROWS_PER_QUADRANT * quadrant : ROWS_PER_QUADRANT * (quadrant + 1), :
+                            ]
+                            .bitcast(I32)
+                            .rearrange("q (j n) -> j q n", j=PLANES_PER_TILE),
+                        )
+
+            def load_span_planes(slab):
+                for quadrant in range(QUADRANTS):
+                    nc.sync.dma_start(
+                        out=span_planes[32 * quadrant : 32 * quadrant + 16, slab, :].bitcast(I32),
+                        in_=w_span_scales[
+                            PLANES_PER_TILE * slab : PLANES_PER_TILE * (slab + 1),
+                            ROWS_PER_QUADRANT * quadrant : ROWS_PER_QUADRANT * (quadrant + 1),
+                            :,
+                        ].bitcast(I32),
+                    )
 
             reduce_words = []
             for unit in range(REDUCE_UNITS):
@@ -139,21 +164,12 @@ def tile_involution_k_kernel(
                         ].bitcast(I32),
                     )
                     unit_words.append(words)
+                    if unit == 0 and g == 0:
+                        load_reduce_planes()
+                    slab = C_PASSES * unit + g - C_PASSES
+                    if 0 <= slab < R_PASSES // PLANES_PER_TILE:
+                        load_span_planes(slab)
                 reduce_words.append(unit_words)
-                if unit == 0:
-                    for g in range(C_PASSES):
-                        for quadrant in range(QUADRANTS):
-                            nc.sync.dma_start(
-                                out=reduce_planes[32 * quadrant : 32 * quadrant + 16, g, :].bitcast(I32),
-                                in_=w_reduce_scales[
-                                    g, ROWS_PER_QUADRANT * quadrant : ROWS_PER_QUADRANT * (quadrant + 1), :
-                                ]
-                                .bitcast(I32)
-                                .rearrange("q (j n) -> j q n", j=PLANES_PER_TILE),
-                            )
-
-            for slab in range(R_PASSES // PLANES_PER_TILE):
-                nc.gpsimd.memset(span_planes[:, slab, :].bitcast(F32), 0.0)
 
             x_masked = keep.tile([P, K, PAIR_TILES, FLAT], F32)
             nc.vector.memset(x_masked[:, :, :, 0:FLAT_PAD], 0.0)
@@ -234,17 +250,6 @@ def tile_involution_k_kernel(
                     in_=window[:].rearrange("n g u p -> n g p u"),
                 )
 
-            for slab in range(R_PASSES // PLANES_PER_TILE):
-                for quadrant in range(QUADRANTS):
-                    nc.sync.dma_start(
-                        out=span_planes[32 * quadrant : 32 * quadrant + 16, slab, :].bitcast(I32),
-                        in_=w_span_scales[
-                            PLANES_PER_TILE * slab : PLANES_PER_TILE * (slab + 1),
-                            ROWS_PER_QUADRANT * quadrant : ROWS_PER_QUADRANT * (quadrant + 1),
-                            :,
-                        ].bitcast(I32),
-                    )
-
             def reduce_product(chunk):
                 raw = early.tile([P, TILES_PER_CHUNK, BANK_F32], F32, bufs=2)
                 for a in range(TILES_PER_CHUNK):
@@ -315,7 +320,8 @@ def tile_involution_k_kernel(
                 if chunk > 0:
                     quantise_red(chunk - 1, red_behind)
                 biased_behind = biased_now
-                shift_image(HEAD_TAPS + chunk, True)
+                for tap in range(HEAD_TAPS + CHUNK_TAPS * chunk, HEAD_TAPS + CHUNK_TAPS * (chunk + 1)):
+                    shift_image(tap, tap % 2 == 0)
             red_behind = rectify_red(biased_behind)
             quantise_red(REDUCE_CHUNKS - 1, red_behind)
             for first_row in range(0, SPAN_BIAS_ROWS, ROWS_PER_BANK):
@@ -325,7 +331,7 @@ def tile_involution_k_kernel(
         products = {}
 
         def rest_of_images(load, loads):
-            left = TAPS - HEAD_TAPS - REDUCE_CHUNKS
+            left = TAPS - HEAD_TAPS - CHUNK_TAPS * REDUCE_CHUNKS
             first_tap = TAPS - left
             for tap in range(first_tap + left * load // loads, first_tap + left * (load + 1) // loads):
                 shift_image(tap, tap % 2 == 0)
@@ -395,23 +401,22 @@ def tile_involution_k_kernel(
             nc.vector.tensor_tensor(out=result[:], in0=summed[:], in1=inverse, op=ALU.mult)
             return result
 
-        def store(c_tile, result):
-            nc.scalar.dma_start(out=out_rows[P * c_tile : P * (c_tile + 1), :], in_=result[:])
+        def store(queue, c_tile, result):
+            queue.dma_start(out=out_rows[P * c_tile : P * (c_tile + 1), :], in_=result[:])
 
         def span_product(block, ready, between_loads):
             width = SPAN_BLOCKS[block]
             first_col = banks[block_banks[block][0]][0]
             for b in block_banks[block]:
                 accs[b] = psum.tile([P, BANK_F32], F32, tag="acc", bufs=ACC_BANKS, name="acc")
-            passes = MAX_PASSES_PER_LOAD
-            while passes * width > STREAM_WORDS:
-                passes //= 2
-            load_passes = [passes] * (R_PASSES // passes)
+            loads = -(-R_PASSES // min(MAX_PASSES_PER_LOAD, STREAM_WORDS // width))
+            load_ends = [R_PASSES * (load + 1) // loads for load in range(loads)]
             if block == len(SPAN_BLOCKS) - 1:
-                load_passes[-1:] = [passes - LAST_PASSES, LAST_PASSES]
-            loads = len(load_passes)
-            for load, passes in enumerate(load_passes):
-                first_pass = sum(load_passes[:load])
+                load_ends[-1:] = [R_PASSES - LAST_PASSES, R_PASSES]
+                loads += 1
+            first_pass = 0
+            for load, end_pass in enumerate(load_ends):
+                passes = end_pass - first_pass
                 words = stream.tile(
                     [P, STREAM_WORDS], U32, tag="words", name="span_words", align_bytes=64
                 )
@@ -421,7 +426,7 @@ def tile_involution_k_kernel(
                         :, first_pass : first_pass + passes, PACK * first_col : PACK * (first_col + width)
                     ].bitcast(I32),
                 )
-                for g in range(first_pass, first_pass + passes):
+                for g in range(first_pass, end_pass):
                     for b in block_banks[block]:
                         bank_col, bank_width = banks[b]
                         first_word = width * (g - first_pass) + bank_col - first_col
@@ -439,6 +444,7 @@ def tile_involution_k_kernel(
                             stop=(g == R_PASSES - 1),
                         )
                 between_loads(load, loads)
+                first_pass = end_pass
             flipped = flip_inverses(ready) if ready else None
             return flipped, [add_taps(c_tile) for c_tile in ready]
 
@@ -531,9 +537,9 @@ def tile_involution_k_kernel(
                 elif block == last_block:
                     ready += multiply(part, (0, TAPS // 2, TAPS))
             for i, c_tile in enumerate(summed_tiles):
-                store(c_tile, scale_sum(sums[i], inverse_rows[:, i, :]))
+                store(nc.scalar if block == last_block else nc.gpsimd, c_tile, scale_sum(sums[i], inverse_rows[:, i, :]))
             waiting = parts[-1]
         flipped = flip_inverses(ready)
         inverse_rows = copy_inverses(len(ready), flipped)
         for i, c_tile in enumerate(ready):
-            store(c_tile, scale_sum(add_taps(c_tile), inverse_rows[:, i, :]))
+            store(nc.scalar, c_tile, scale_sum(add_taps(c_tile), inverse_rows[:, i, :]))

@@ -27,8 +27,6 @@ CH_PER_GROUP = C // GROUPS
 K = 5
 PAD = K // 2
 TAPS = K * K
-CHUNK_TAPS = 2
-HEAD_TAPS = 8
 O = GROUPS * TAPS
 
 C_PASSES = C // K_PASS
@@ -40,13 +38,13 @@ GROUPS_PER_TILE = P // CH_PER_GROUP
 MAX_READY = BANK_F32 // PIX
 
 STREAM_WORDS = 2048
-STREAM_BUFS = 8
+STREAM_BUFS = 9
 REDUCE_UNITS = R // STREAM_WORDS
 REDUCE_CHUNK = 1024
 REDUCE_CHUNKS = R // REDUCE_CHUNK
 TILES_PER_CHUNK = REDUCE_CHUNK // BANK_F32
 
-SPAN_BLOCKS = [640, 1024, 768, 384, 256, 128]
+SPAN_BLOCKS = [1024, 1024, 512, 256, 256, 128]
 MM_WIDTHS = [512, 256, 128]
 MAX_PASSES_PER_LOAD = 8
 LAST_PASSES = 2
@@ -111,6 +109,8 @@ def tile_involution_k_kernel(
             x_codes = early.tile([P, C_PASSES, PIX], U32, align_bytes=64)
             reduce_planes = early.tile([P, C_PASSES, REDUCE_PLANE_COLS], U8, align_bytes=64)
             nc.vector.memset(reduce_planes[:].rearrange("p g n -> p (g n)").bitcast(I32), 0)
+            for slab in range(R_PASSES // PLANES_PER_TILE):
+                nc.vector.memset(span_planes[:, slab, :].bitcast(I32), 0)
             reduce_bias_rows = early.tile([P, K_PASS], BF16)
             span_bias_rows = early.tile([P, P], BF16)
             nc.gpsimd.memset(reduce_bias_rows[:], 0.0)
@@ -123,9 +123,6 @@ def tile_involution_k_kernel(
             )
             make_identity(nc, ident_f32[:])
             make_identity(nc, ident_bf16[:])
-
-            for slab in range(R_PASSES // PLANES_PER_TILE):
-                nc.gpsimd.memset(span_planes[:, slab, :].bitcast(F32), 0.0)
 
             def load_reduce_planes():
                 for g in range(C_PASSES):
@@ -150,6 +147,9 @@ def tile_involution_k_kernel(
                         ].bitcast(I32),
                     )
 
+            load_reduce_planes()
+            for slab in range(R_PASSES // PLANES_PER_TILE):
+                load_span_planes(slab)
             reduce_words = []
             for unit in range(REDUCE_UNITS):
                 unit_words = []
@@ -164,14 +164,9 @@ def tile_involution_k_kernel(
                         ].bitcast(I32),
                     )
                     unit_words.append(words)
-                    if unit == 0 and g == 0:
-                        load_reduce_planes()
-                    slab = C_PASSES * unit + g - C_PASSES
-                    if 0 <= slab < R_PASSES // PLANES_PER_TILE:
-                        load_span_planes(slab)
                 reduce_words.append(unit_words)
 
-            x_masked = keep.tile([P, K, PAIR_TILES, FLAT], F32)
+            x_masked = early.tile([P, K, PAIR_TILES, FLAT], F32)
             nc.vector.memset(x_masked[:, :, :, 0:FLAT_PAD], 0.0)
             nc.vector.memset(x_masked[:, :, :, FLAT_PAD + PIX : FLAT], 0.0)
             for j in range(K):
@@ -234,7 +229,7 @@ def tile_involution_k_kernel(
                     out=span_bias[:, P * first_row : P * (first_row + rows)], in_=bank[:, : P * rows]
                 )
 
-            def shift_image(tap, by_scalar):
+            def shift_image(tap):
                 i, j = divmod(tap, K)
                 first = FLAT_PAD + (i - PAD) * W + (j - PAD)
                 window = psum.tile([P, C_PASSES, PAIRS, P], F32, tag="scratch", bufs=SCRATCH_BANKS)
@@ -244,7 +239,7 @@ def tile_involution_k_kernel(
                         x_masked[:, j, pt, first : first + PIX],
                         ident_f32[:],
                     )
-                copy_out = nc.scalar.copy if by_scalar else nc.vector.tensor_copy
+                copy_out = nc.scalar.copy if tap % 2 == 0 else nc.vector.tensor_copy
                 copy_out(
                     out=shifted[:, tap, :].bitcast(F32).rearrange("n (g p u) -> n g p u", g=C_PASSES, u=PAIRS),
                     in_=window[:].rearrange("n g u p -> n g p u"),
@@ -306,8 +301,10 @@ def tile_involution_k_kernel(
                     in_=red_grouped[:].rearrange("q a n t -> q (a n t)"),
                 )
 
-            for tap in range(HEAD_TAPS):
-                shift_image(tap, tap % 2 == 0)
+            for tap in range(TAPS):
+                shift_image(tap)
+            for first_row in range(0, SPAN_BIAS_ROWS, ROWS_PER_BANK):
+                spread_span_bias(first_row, min(ROWS_PER_BANK, SPAN_BIAS_ROWS - first_row))
             raw_ahead = reduce_product(0)
             biased_behind = None
             for chunk in range(REDUCE_CHUNKS):
@@ -320,24 +317,11 @@ def tile_involution_k_kernel(
                 if chunk > 0:
                     quantise_red(chunk - 1, red_behind)
                 biased_behind = biased_now
-                for tap in range(HEAD_TAPS + CHUNK_TAPS * chunk, HEAD_TAPS + CHUNK_TAPS * (chunk + 1)):
-                    shift_image(tap, tap % 2 == 0)
             red_behind = rectify_red(biased_behind)
             quantise_red(REDUCE_CHUNKS - 1, red_behind)
-            for first_row in range(0, SPAN_BIAS_ROWS, ROWS_PER_BANK):
-                spread_span_bias(first_row, min(ROWS_PER_BANK, SPAN_BIAS_ROWS - first_row))
 
         late = ctx.enter_context(tc.tile_pool(name="late", bufs=2))
         products = {}
-
-        def rest_of_images(load, loads):
-            left = TAPS - HEAD_TAPS - CHUNK_TAPS * REDUCE_CHUNKS
-            first_tap = TAPS - left
-            for tap in range(first_tap + left * load // loads, first_tap + left * (load + 1) // loads):
-                shift_image(tap, tap % 2 == 0)
-
-        def nothing(load, loads):
-            pass
 
         banks = []
         block_banks = []
@@ -401,10 +385,10 @@ def tile_involution_k_kernel(
             nc.vector.tensor_tensor(out=result[:], in0=summed[:], in1=inverse, op=ALU.mult)
             return result
 
-        def store(queue, c_tile, result):
-            queue.dma_start(out=out_rows[P * c_tile : P * (c_tile + 1), :], in_=result[:])
+        def store(c_tile, result):
+            nc.scalar.dma_start(out=out_rows[P * c_tile : P * (c_tile + 1), :], in_=result[:])
 
-        def span_product(block, ready, between_loads):
+        def span_product(block, ready):
             width = SPAN_BLOCKS[block]
             first_col = banks[block_banks[block][0]][0]
             for b in block_banks[block]:
@@ -443,7 +427,6 @@ def tile_involution_k_kernel(
                             start=(g == 0),
                             stop=(g == R_PASSES - 1),
                         )
-                between_loads(load, loads)
                 first_pass = end_pass
             flipped = flip_inverses(ready) if ready else None
             return flipped, [add_taps(c_tile) for c_tile in ready]
@@ -518,7 +501,7 @@ def tile_involution_k_kernel(
         waiting = None
         last_block = len(SPAN_BLOCKS) - 1
         for block in range(len(SPAN_BLOCKS)):
-            flipped, sums = span_product(block, ready, rest_of_images if block == 0 else nothing)
+            flipped, sums = span_product(block, ready)
             for b in block_banks[block]:
                 add_bias(b)
             parts = block_parts[block]
@@ -537,9 +520,9 @@ def tile_involution_k_kernel(
                 elif block == last_block:
                     ready += multiply(part, (0, TAPS // 2, TAPS))
             for i, c_tile in enumerate(summed_tiles):
-                store(nc.scalar if block == last_block else nc.gpsimd, c_tile, scale_sum(sums[i], inverse_rows[:, i, :]))
+                store(c_tile, scale_sum(sums[i], inverse_rows[:, i, :]))
             waiting = parts[-1]
         flipped = flip_inverses(ready)
         inverse_rows = copy_inverses(len(ready), flipped)
         for i, c_tile in enumerate(ready):
-            store(nc.scalar, c_tile, scale_sum(add_taps(c_tile), inverse_rows[:, i, :]))
+            store(c_tile, scale_sum(add_taps(c_tile), inverse_rows[:, i, :]))

@@ -48,13 +48,13 @@ SPAN_BLOCKS = [1024, 1024, 512, 256, 256, 128]
 MM_WIDTHS = [512, 256, 128]
 MAX_PASSES_PER_LOAD = 8
 LAST_PASSES = 2
-PART_GROUPS = 16
+PART_GROUPS = 8
 LAST_TILE_GROUPS = 6
-HALF_TILE = PART_GROUPS // 2
-PART_BUFS = 4
+LAST_BLOCK_GROUPS = 3
+PART_BUFS = 6
 
 PLANES_PER_TILE = 4
-QUADRANTS = 4
+QUADRANT_ORDER = [0, 2, 1, 3]
 ROWS_PER_QUADRANT = 4
 REDUCE_PLANE_COLS = R // PLANES_PER_TILE
 
@@ -100,17 +100,18 @@ def tile_involution_k_kernel(
             nc.scalar.dma_start(
                 out=x_by_word[:], in_=image.rearrange("(g p t) h w -> p g t (h w)", p=P, t=PACK)
             )
-            one = early.tile([P, 1], F32)
-            nc.vector.memset(one[:], 1.0)
-            exp_of_one = early.tile([P, 1], F32)
-            nc.scalar.activation(out=exp_of_one[:], in_=one[:], func=ACT.Exp)
 
             x_scales = early.tile([P, C_PASSES, PIX], U8, align_bytes=64)
             x_codes = early.tile([P, C_PASSES, PIX], U32, align_bytes=64)
             reduce_planes = early.tile([P, C_PASSES, REDUCE_PLANE_COLS], U8, align_bytes=64)
-            nc.vector.memset(reduce_planes[:].rearrange("p g n -> p (g n)").bitcast(I32), 0)
+            for g in range(C_PASSES):
+                nc.vector.memset(reduce_planes[:, g, :].bitcast(I32), 0)
             for slab in range(R_PASSES // PLANES_PER_TILE):
                 nc.vector.memset(span_planes[:, slab, :].bitcast(I32), 0)
+            one = early.tile([P, 1], F32)
+            nc.vector.memset(one[:], 1.0)
+            exp_of_one = early.tile([P, 1], F32)
+            nc.scalar.activation(out=exp_of_one[:], in_=one[:], func=ACT.Exp)
             reduce_bias_rows = early.tile([P, K_PASS], BF16)
             span_bias_rows = early.tile([P, P], BF16)
             nc.gpsimd.memset(reduce_bias_rows[:], 0.0)
@@ -126,7 +127,7 @@ def tile_involution_k_kernel(
 
             def load_reduce_planes():
                 for g in range(C_PASSES):
-                    for quadrant in range(QUADRANTS):
+                    for quadrant in QUADRANT_ORDER:
                         nc.sync.dma_start(
                             out=reduce_planes[32 * quadrant : 32 * quadrant + 16, g, :].bitcast(I32),
                             in_=w_reduce_scales[
@@ -137,7 +138,7 @@ def tile_involution_k_kernel(
                         )
 
             def load_span_planes(slab):
-                for quadrant in range(QUADRANTS):
+                for quadrant in QUADRANT_ORDER:
                     nc.sync.dma_start(
                         out=span_planes[32 * quadrant : 32 * quadrant + 16, slab, :].bitcast(I32),
                         in_=w_span_scales[
@@ -341,12 +342,13 @@ def tile_involution_k_kernel(
             last_col, last_width = banks[numbers[-1]]
             end_group = (last_col + last_width) // TAPS
             if end_group < GROUPS - GROUPS_PER_TILE:
-                end_group -= end_group % HALF_TILE
+                end_group -= end_group % PART_GROUPS
             parts = []
             while group < end_group:
-                part_end = min(end_group, PART_GROUPS * (group // PART_GROUPS + 1))
+                size = PART_GROUPS
                 if group >= GROUPS - GROUPS_PER_TILE:
-                    part_end = min(part_end, group + LAST_TILE_GROUPS)
+                    size = LAST_TILE_GROUPS if end_group < GROUPS else LAST_BLOCK_GROUPS
+                part_end = min(end_group, group + size)
                 parts.append((group, part_end))
                 group = part_end
             block_parts.append(parts)
@@ -521,7 +523,10 @@ def tile_involution_k_kernel(
                     ready += multiply(part, (0, TAPS // 2, TAPS))
             for i, c_tile in enumerate(summed_tiles):
                 store(c_tile, scale_sum(sums[i], inverse_rows[:, i, :]))
-            waiting = parts[-1]
+            if block == 0:
+                ready += multiply(parts[-1])
+            else:
+                waiting = parts[-1]
         flipped = flip_inverses(ready)
         inverse_rows = copy_inverses(len(ready), flipped)
         for i, c_tile in enumerate(ready):

@@ -44,13 +44,23 @@ REDUCE_CHUNK = 1024
 REDUCE_CHUNKS = R // REDUCE_CHUNK
 TILES_PER_CHUNK = REDUCE_CHUNK // BANK_F32
 
-SPAN_BLOCKS = [1024, 1024, 512, 256, 256, 128]
+SPAN_STAGES = [
+    [(0, 1024, 0, 16)],
+    [(1024, 1024, 0, 8), (1024, 512, 8, 16)],
+    [(1536, 512, 8, 16)],
+    [(2048, 512, 0, 16)],
+    [(2560, 256, 0, 16)],
+    [(2816, 256, 0, 16)],
+    [(3072, 128, 0, 16)],
+]
+STAGE_ENDS = [entries[-1][0] + entries[-1][1] for entries in SPAN_STAGES]
+STAGES = len(SPAN_STAGES)
 MM_WIDTHS = [512, 256, 128]
 MAX_PASSES_PER_LOAD = 8
 LAST_PASSES = 2
 PART_GROUPS = 8
 LAST_TILE_GROUPS = 6
-LAST_BLOCK_GROUPS = 3
+LAST_STAGE_GROUPS = 3
 PART_BUFS = 6
 
 PLANES_PER_TILE = 4
@@ -324,43 +334,41 @@ def tile_involution_k_kernel(
         late = ctx.enter_context(tc.tile_pool(name="late", bufs=2))
         products = {}
 
-        banks = []
-        block_banks = []
-        for width in SPAN_BLOCKS:
-            numbers = []
-            left = width
-            for mm_width in MM_WIDTHS:
-                while left >= mm_width:
-                    first_col = banks[-1][0] + banks[-1][1] if banks else 0
-                    numbers.append(len(banks))
-                    banks.append((first_col, mm_width))
-                    left -= mm_width
-            block_banks.append(numbers)
-        block_parts = []
+        stage_banks = []
+        first_col = 0
+        for end_col in STAGE_ENDS:
+            stage_banks.append([])
+            while first_col < end_col:
+                width = max(w for w in MM_WIDTHS if w <= end_col - first_col)
+                stage_banks[-1].append((first_col, width))
+                first_col += width
+        banks = [bank for numbers in stage_banks for bank in numbers]
+        stage_parts = []
         group = 0
-        for numbers in block_banks:
-            last_col, last_width = banks[numbers[-1]]
-            end_group = (last_col + last_width) // TAPS
+        for end_col in STAGE_ENDS:
+            end_group = end_col // TAPS
             if end_group < GROUPS - GROUPS_PER_TILE:
                 end_group -= end_group % PART_GROUPS
             parts = []
             while group < end_group:
                 size = PART_GROUPS
                 if group >= GROUPS - GROUPS_PER_TILE:
-                    size = LAST_TILE_GROUPS if end_group < GROUPS else LAST_BLOCK_GROUPS
+                    size = LAST_TILE_GROUPS if end_group < GROUPS else LAST_STAGE_GROUPS
                 part_end = min(end_group, group + size)
                 parts.append((group, part_end))
                 group = part_end
-            block_parts.append(parts)
+            stage_parts.append(parts)
         accs = {}
         exponentials = {}
         totals = {}
         group_inverses = {}
         inverses = {}
 
-        def add_taps(c_tile):
-            summed = psum.tile([P, PIX], F32, tag="scratch", bufs=SCRATCH_BANKS)
-            for tap in range(TAPS):
+        def begin_sum():
+            return psum.tile([P, PIX], F32, tag="scratch", bufs=SCRATCH_BANKS, name="summed")
+
+        def add_taps(summed, c_tile, taps):
+            for tap in taps:
                 nc.tensor.matmul(
                     out=summed[:],
                     lhsT=products[c_tile][:, tap, :],
@@ -369,7 +377,6 @@ def tile_involution_k_kernel(
                     stop=(tap == TAPS - 1),
                     is_transpose=True,
                 )
-            return summed
 
         def flip_inverses(c_tiles):
             flipped = psum.tile([P, MAX_READY, PIX], F32, tag="scratch", bufs=SCRATCH_BANKS)
@@ -390,51 +397,48 @@ def tile_involution_k_kernel(
         def store(c_tile, result):
             nc.scalar.dma_start(out=out_rows[P * c_tile : P * (c_tile + 1), :], in_=result[:])
 
-        def span_product(block, ready):
-            width = SPAN_BLOCKS[block]
-            first_col = banks[block_banks[block][0]][0]
-            for b in block_banks[block]:
-                accs[b] = psum.tile([P, BANK_F32], F32, tag="acc", bufs=ACC_BANKS, name="acc")
-            loads = -(-R_PASSES // min(MAX_PASSES_PER_LOAD, STREAM_WORDS // width))
-            load_ends = [R_PASSES * (load + 1) // loads for load in range(loads)]
-            if block == len(SPAN_BLOCKS) - 1:
-                load_ends[-1:] = [R_PASSES - LAST_PASSES, R_PASSES]
-                loads += 1
-            first_pass = 0
-            for load, end_pass in enumerate(load_ends):
-                passes = end_pass - first_pass
-                words = stream.tile(
-                    [P, STREAM_WORDS], U32, tag="words", name="span_words", align_bytes=64
-                )
-                nc.sync.dma_start(
-                    out=words[:, : passes * width].rearrange("p (g n) -> p g n", n=width).bitcast(I32),
-                    in_=span_bytes[
-                        :, first_pass : first_pass + passes, PACK * first_col : PACK * (first_col + width)
-                    ].bitcast(I32),
-                )
-                for g in range(first_pass, end_pass):
-                    for b in block_banks[block]:
-                        bank_col, bank_width = banks[b]
-                        first_word = width * (g - first_pass) + bank_col - first_col
-                        nc.tensor.matmul_mx(
-                            out=accs[b][:, :bank_width],
-                            lhsT=red_codes[:, g, :].bitcast(FP8X4),
-                            lhsT_scale=red_scales[:, g, :],
-                            rhs=words[:, first_word : first_word + bank_width].bitcast(FP8X4),
-                            rhs_scale=span_planes[
-                                ROWS_PER_QUADRANT * (g % PLANES_PER_TILE) : P,
-                                g // PLANES_PER_TILE,
-                                bank_col : bank_col + bank_width,
-                            ],
-                            start=(g == 0),
-                            stop=(g == R_PASSES - 1),
-                        )
-                first_pass = end_pass
-            flipped = flip_inverses(ready) if ready else None
-            return flipped, [add_taps(c_tile) for c_tile in ready]
+        def span_product(stage):
+            for first_col, width, pass_start, pass_end in SPAN_STAGES[stage]:
+                entry_banks = [b for b in banks if first_col <= b[0] < first_col + width]
+                if pass_start == 0:
+                    for b in entry_banks:
+                        accs[b] = psum.tile([P, BANK_F32], F32, tag="acc", bufs=ACC_BANKS, name="acc")
+                step = min(MAX_PASSES_PER_LOAD, STREAM_WORDS // width)
+                load_ends = list(range(pass_start + step, pass_end + 1, step))
+                if stage == STAGES - 1:
+                    load_ends[-1:] = [pass_end - LAST_PASSES, pass_end]
+                first_pass = pass_start
+                for end_pass in load_ends:
+                    passes = end_pass - first_pass
+                    words = stream.tile(
+                        [P, STREAM_WORDS], U32, tag="words", name="span_words", align_bytes=64
+                    )
+                    nc.sync.dma_start(
+                        out=words[:, : passes * width].rearrange("p (g n) -> p g n", n=width).bitcast(I32),
+                        in_=span_bytes[
+                            :, first_pass:end_pass, PACK * first_col : PACK * (first_col + width)
+                        ].bitcast(I32),
+                    )
+                    for g in range(first_pass, end_pass):
+                        for bank_col, bank_width in entry_banks:
+                            first_word = width * (g - first_pass) + bank_col - first_col
+                            nc.tensor.matmul_mx(
+                                out=accs[bank_col, bank_width][:, :bank_width],
+                                lhsT=red_codes[:, g, :].bitcast(FP8X4),
+                                lhsT_scale=red_scales[:, g, :],
+                                rhs=words[:, first_word : first_word + bank_width].bitcast(FP8X4),
+                                rhs_scale=span_planes[
+                                    ROWS_PER_QUADRANT * (g % PLANES_PER_TILE) : P,
+                                    g // PLANES_PER_TILE,
+                                    bank_col : bank_col + bank_width,
+                                ],
+                                start=(g == 0),
+                                stop=(g == R_PASSES - 1),
+                            )
+                    first_pass = end_pass
 
         def add_bias(b):
-            first_col, width = banks[b]
+            first_col, width = b
             cols = slice(first_col, first_col + width)
             nc.vector.tensor_tensor(
                 out=kern[:, cols], in0=accs[b][:, :width], in1=span_bias[:, cols], op=ALU.add
@@ -501,33 +505,39 @@ def tile_involution_k_kernel(
 
         ready = []
         waiting = None
-        last_block = len(SPAN_BLOCKS) - 1
-        for block in range(len(SPAN_BLOCKS)):
-            flipped, sums = span_product(block, ready)
-            for b in block_banks[block]:
+        for stage in range(STAGES):
+            is_last = stage == STAGES - 1
+            span_product(stage)
+            to_sum = ready if stage != STAGES - 2 else []
+            ready = [c_tile for c_tile in ready if c_tile not in to_sum]
+            flipped = flip_inverses(to_sum) if to_sum else None
+            sums = []
+            for c_tile in to_sum:
+                sums.append(begin_sum())
+                add_taps(sums[-1], c_tile, range(TAPS))
+            for b in stage_banks[stage]:
                 add_bias(b)
-            parts = block_parts[block]
+            parts = stage_parts[stage]
             for part in parts:
                 exponentiate(part)
-            inverse_rows = copy_inverses(len(ready), flipped) if ready else None
-            summed_tiles = ready
-            ready = []
+            inverse_rows = copy_inverses(len(to_sum), flipped) if to_sum else None
             if waiting:
                 ready += multiply(waiting)
+            waiting = None
             for part in parts:
                 invert(part)
                 spread_inverse(part)
-                if part != parts[-1]:
+                if part != parts[-1] or stage == 0:
                     ready += multiply(part)
-                elif block == last_block:
+                elif is_last:
                     ready += multiply(part, (0, TAPS // 2, TAPS))
-            for i, c_tile in enumerate(summed_tiles):
+                else:
+                    waiting = part
+            for i, c_tile in enumerate(to_sum):
                 store(c_tile, scale_sum(sums[i], inverse_rows[:, i, :]))
-            if block == 0:
-                ready += multiply(parts[-1])
-            else:
-                waiting = parts[-1]
-        flipped = flip_inverses(ready)
-        inverse_rows = copy_inverses(len(ready), flipped)
-        for i, c_tile in enumerate(ready):
-            store(c_tile, scale_sum(add_taps(c_tile), inverse_rows[:, i, :]))
+        c_tile = ready[-1]
+        summed = begin_sum()
+        add_taps(summed, c_tile, range(TAPS // 2))
+        inverse_rows = copy_inverses(1, flip_inverses([c_tile]))
+        add_taps(summed, c_tile, range(TAPS // 2, TAPS))
+        store(c_tile, scale_sum(summed, inverse_rows[:, 0, :]))

@@ -27,6 +27,7 @@ CH_PER_GROUP = C // GROUPS
 K = 5
 PAD = K // 2
 TAPS = K * K
+WARM_TAPS = 9
 O = GROUPS * TAPS
 
 C_PASSES = C // K_PASS
@@ -367,8 +368,16 @@ def tile_involution_k_kernel(
         def begin_sum():
             return psum.tile([P, PIX], F32, tag="scratch", bufs=SCRATCH_BANKS, name="summed")
 
-        def add_taps(summed, c_tile, taps):
+        def add_taps(summed, c_tile, taps, warm_bank):
             for tap in taps:
+                if warm_bank is not None and tap % WARM_TAPS == 0:
+                    nc.tensor.matmul(
+                        out=warm_bank[:],
+                        lhsT=ident_bf16[:],
+                        rhs=shifted[:, 0, 0:BANK_F32],
+                        start=True,
+                        stop=True,
+                    )
                 nc.tensor.matmul(
                     out=summed[:],
                     lhsT=products[c_tile][:, tap, :],
@@ -394,8 +403,8 @@ def tile_involution_k_kernel(
             nc.vector.tensor_tensor(out=result[:], in0=summed[:], in1=inverse, op=ALU.mult)
             return result
 
-        def store(c_tile, result):
-            nc.scalar.dma_start(out=out_rows[P * c_tile : P * (c_tile + 1), :], in_=result[:])
+        def store(queue, c_tile, result):
+            queue.dma_start(out=out_rows[P * c_tile : P * (c_tile + 1), :], in_=result[:])
 
         def span_product(stage):
             for first_col, width, pass_start, pass_end in SPAN_STAGES[stage]:
@@ -404,7 +413,7 @@ def tile_involution_k_kernel(
                     for b in entry_banks:
                         accs[b] = psum.tile([P, BANK_F32], F32, tag="acc", bufs=ACC_BANKS, name="acc")
                 step = min(MAX_PASSES_PER_LOAD, STREAM_WORDS // width)
-                load_ends = list(range(pass_start + step, pass_end + 1, step))
+                load_ends = list(range(pass_start + step, pass_end, step)) + [pass_end]
                 if stage == STAGES - 1:
                     load_ends[-1:] = [pass_end - LAST_PASSES, pass_end]
                 first_pass = pass_start
@@ -508,13 +517,16 @@ def tile_involution_k_kernel(
         for stage in range(STAGES):
             is_last = stage == STAGES - 1
             span_product(stage)
-            to_sum = ready if stage != STAGES - 2 else []
-            ready = [c_tile for c_tile in ready if c_tile not in to_sum]
+            to_sum = ready
+            ready = []
+            warm_bank = None
+            if stage >= STAGES - 2:
+                warm_bank = psum.tile([P, BANK_F32], F32, tag="acc", bufs=ACC_BANKS)
             flipped = flip_inverses(to_sum) if to_sum else None
             sums = []
             for c_tile in to_sum:
                 sums.append(begin_sum())
-                add_taps(sums[-1], c_tile, range(TAPS))
+                add_taps(sums[-1], c_tile, range(TAPS), warm_bank)
             for b in stage_banks[stage]:
                 add_bias(b)
             parts = stage_parts[stage]
@@ -534,10 +546,10 @@ def tile_involution_k_kernel(
                 else:
                     waiting = part
             for i, c_tile in enumerate(to_sum):
-                store(c_tile, scale_sum(sums[i], inverse_rows[:, i, :]))
+                store(nc.scalar, c_tile, scale_sum(sums[i], inverse_rows[:, i, :]))
         c_tile = ready[-1]
         summed = begin_sum()
-        add_taps(summed, c_tile, range(TAPS // 2))
+        add_taps(summed, c_tile, range(TAPS // 2), warm_bank)
         inverse_rows = copy_inverses(1, flip_inverses([c_tile]))
-        add_taps(summed, c_tile, range(TAPS // 2, TAPS))
-        store(c_tile, scale_sum(summed, inverse_rows[:, 0, :]))
+        add_taps(summed, c_tile, range(TAPS // 2, TAPS), None)
+        store(nc.sync, c_tile, scale_sum(summed, inverse_rows[:, 0, :]))

from contextlib import ExitStack

import concourse.mybir as mybir
from concourse.masks import make_identity

BF16 = mybir.dt.bfloat16
F32 = mybir.dt.float32
I32 = mybir.dt.int32
U32 = mybir.dt.uint32
U8 = mybir.dt.uint8
FP8X4 = mybir.dt.float8_e4m3fn_x4
ALU = mybir.AluOpType
ACT = mybir.ActivationFunctionType
AXIS_X = mybir.AxisListType.X

P = 128
PACK = 4
K_PASS = P * PACK
BANK_F32 = 512
BANK_BF16 = 1024

C, H, W = 1024, 8, 16
PIX = H * W
R = 8192
GROUPS = 128
CH_PER_GROUP = C // GROUPS
K = 5
PAD = K // 2
TAPS = K * K
WARM_TAPS = 9
O = GROUPS * TAPS

C_PASSES = C // K_PASS
R_PASSES = R // K_PASS
C_TILES = C // P
PAIRS = PACK // 2
PAIR_TILES = C_PASSES * PAIRS
GROUPS_PER_TILE = P // CH_PER_GROUP
MAX_READY = BANK_F32 // PIX

STREAM_WORDS = 2048
STREAM_BUFS = 9
REDUCE_UNITS = R // STREAM_WORDS
REDUCE_CHUNK = 1024
REDUCE_CHUNKS = R // REDUCE_CHUNK
TILES_PER_CHUNK = REDUCE_CHUNK // BANK_F32

SPAN_STAGES = [
    [(0, 1024, 0, 16)],
    [(1024, 1024, 0, 8), (1024, 512, 8, 16)],
    [(1536, 512, 8, 16)],
    [(2048, 512, 0, 16)],
    [(2560, 256, 0, 16)],
    [(2816, 256, 0, 16)],
    [(3072, 128, 0, 16)],
]
STAGE_ENDS = [entries[-1][0] + entries[-1][1] for entries in SPAN_STAGES]
STAGES = len(SPAN_STAGES)
MM_WIDTHS = [512, 256, 128]
MAX_PASSES_PER_LOAD = 8
LAST_PASSES = 2
PART_GROUPS = 8
LAST_TILE_GROUPS = 6
LAST_STAGE_GROUPS = 3
PART_BUFS = 6

PLANES_PER_TILE = 4
QUADRANT_ORDER = [0, 2, 1, 3]
ROWS_PER_QUADRANT = 4
REDUCE_PLANE_COLS = R // PLANES_PER_TILE

SPAN_BIAS_ROWS = O // P
ROWS_PER_BANK = BANK_BF16 // P

FLAT_PAD = PAD * W + PAD
FLAT = FLAT_PAD + PIX + FLAT_PAD

SCRATCH_BANKS = 4
ACC_BANKS = 4
PRODUCT_BUFS = 4

FLOPS = 2 * PIX * (C * R + R * O) + 2 * TAPS * C * PIX


def tile_involution_k_kernel(
    tc, x, w_reduce_words, w_reduce_scales, b_reduce, w_span_words, w_span_scales, b_span, out
):
    nc = tc.nc
    image = x[0]
    out_rows = out[0].rearrange("c h w -> c (h w)")
    reduce_bytes = w_reduce_words.rearrange("g p n t -> p g (n t)")
    span_bytes = w_span_words.rearrange("g p n t -> p g (n t)")

    with ExitStack() as ctx:
        keep = ctx.enter_context(tc.tile_pool(name="keep", bufs=1))
        stream = ctx.enter_context(tc.tile_pool(name="stream", bufs=STREAM_BUFS))
        psum = ctx.enter_context(tc.psum_pool(name="psum", bufs=1))
        ctx.enter_context(tc.manual_schedule())

        ident_bf16 = keep.tile([P, P], BF16)
        ident_f32 = keep.tile([P, P], F32)
        span_planes = keep.tile([P, R_PASSES // PLANES_PER_TILE, O], U8, align_bytes=64)
        red_codes = keep.tile([P, R_PASSES, PIX], U32, align_bytes=64)
        red_scales = keep.tile([P, R_PASSES, PIX], U8, align_bytes=64)
        span_bias = keep.tile([P, O], BF16)
        shifted = keep.tile([P, TAPS, C], BF16)
        kern = keep.tile([P, O], F32)

        with tc.tile_pool(name="early", bufs=1) as early:
            x_by_word = early.tile([P, C_PASSES, PACK, PIX], BF16)
            nc.scalar.dma_start(
                out=x_by_word[:], in_=image.rearrange("(g p t) h w -> p g t (h w)", p=P, t=PACK)
            )

            x_scales = early.tile([P, C_PASSES, PIX], U8, align_bytes=64)
            x_codes = early.tile([P, C_PASSES, PIX], U32, align_bytes=64)
            reduce_planes = early.tile([P, C_PASSES, REDUCE_PLANE_COLS], U8, align_bytes=64)
            for g in range(C_PASSES):
                nc.vector.memset(reduce_planes[:, g, :].bitcast(I32), 0)
            for slab in range(R_PASSES // PLANES_PER_TILE):
                nc.vector.memset(span_planes[:, slab, :].bitcast(I32), 0)
            one = early.tile([P, 1], F32)
            nc.vector.memset(one[:], 1.0)
            exp_of_one = early.tile([P, 1], F32)
            nc.scalar.activation(out=exp_of_one[:], in_=one[:], func=ACT.Exp)
            reduce_bias_rows = early.tile([P, K_PASS], BF16)
            span_bias_rows = early.tile([P, P], BF16)
            nc.gpsimd.memset(reduce_bias_rows[:], 0.0)
            nc.gpsimd.memset(span_bias_rows[:], 0.0)
            nc.gpsimd.dma_start(
                out=reduce_bias_rows[0:R_PASSES, :], in_=b_reduce.rearrange("(m n) -> m n", n=K_PASS)
            )
            nc.gpsimd.dma_start(
                out=span_bias_rows[0:SPAN_BIAS_ROWS, :], in_=b_span.rearrange("(m n) -> m n", n=P)
            )
            make_identity(nc, ident_f32[:])
            make_identity(nc, ident_bf16[:])

            def load_reduce_planes():
                for g in range(C_PASSES):
                    for quadrant in QUADRANT_ORDER:
                        nc.sync.dma_start(
                            out=reduce_planes[32 * quadrant : 32 * quadrant + 16, g, :].bitcast(I32),
                            in_=w_reduce_scales[
                                g, ROWS_PER_QUADRANT * quadrant : ROWS_PER_QUADRANT * (quadrant + 1), :
                            ]
                            .bitcast(I32)
                            .rearrange("q (j n) -> j q n", j=PLANES_PER_TILE),
                        )

            def load_span_planes(slab):
                for quadrant in QUADRANT_ORDER:
                    nc.sync.dma_start(
                        out=span_planes[32 * quadrant : 32 * quadrant + 16, slab, :].bitcast(I32),
                        in_=w_span_scales[
                            PLANES_PER_TILE * slab : PLANES_PER_TILE * (slab + 1),
                            ROWS_PER_QUADRANT * quadrant : ROWS_PER_QUADRANT * (quadrant + 1),
                            :,
                        ].bitcast(I32),
                    )

            load_reduce_planes()
            for slab in range(R_PASSES // PLANES_PER_TILE):
                load_span_planes(slab)
            reduce_words = []
            for unit in range(REDUCE_UNITS):
                unit_words = []
                for g in range(C_PASSES):
                    words = stream.tile(
                        [P, STREAM_WORDS], U32, tag="words", name="reduce_words", align_bytes=64
                    )
                    nc.sync.dma_start(
                        out=words[:].bitcast(I32),
                        in_=reduce_bytes[
                            :, g, PACK * STREAM_WORDS * unit : PACK * STREAM_WORDS * (unit + 1)
                        ].bitcast(I32),
                    )
                    unit_words.append(words)
                reduce_words.append(unit_words)

            x_masked = early.tile([P, K, PAIR_TILES, FLAT], F32)
            nc.vector.memset(x_masked[:, :, :, 0:FLAT_PAD], 0.0)
            nc.vector.memset(x_masked[:, :, :, FLAT_PAD + PIX : FLAT], 0.0)
            for j in range(K):
                outside = slice(W + j - PAD, W) if j < PAD else slice(0, j - PAD)
                if j != PAD:
                    nc.vector.memset(
                        x_masked[:, j, :, FLAT_PAD : FLAT_PAD + PIX].rearrange("p a (h w) -> p a h w", w=W)[
                            :, :, :, outside
                        ],
                        0.0,
                    )

            x_grouped = early.tile([P, C_PASSES, PIX, PACK], BF16, align_bytes=64)
            nc.vector.tensor_copy(out=x_grouped[:], in_=x_by_word[:].rearrange("p g t n -> p g n t"))
            nc.vector.quantize_mx(
                out=x_codes[:].rearrange("p g n -> p (g n)").bitcast(FP8X4),
                scales=x_scales[:].rearrange("p g n -> p (g n)"),
                in_=x_grouped[:].rearrange("p g n t -> p (g n t)"),
            )
            for j in range(K):
                lo = max(0, j - PAD)
                hi = W + min(0, j - PAD)
                for g in range(C_PASSES):
                    nc.vector.tensor_copy(
                        out=x_masked[:, j, PAIRS * g : PAIRS * (g + 1), FLAT_PAD : FLAT_PAD + PIX].rearrange(
                            "p u (h w) -> p u h w", w=W
                        )[:, :, :, lo:hi],
                        in_=x_grouped[:, g, :, :]
                        .rearrange("p n t -> p (n t)")
                        .bitcast(F32)
                        .rearrange("p (h w u) -> p u h w", w=W, u=PAIRS)[:, :, :, lo:hi],
                    )

            reduce_bias = early.tile([P, R_PASSES, PACK], F32)
            bias_flipped = psum.tile([P, PACK, P], BF16, tag="scratch", bufs=SCRATCH_BANKS)
            for t in range(PACK):
                nc.tensor.transpose(
                    bias_flipped[:, t, :], reduce_bias_rows[:, t::PACK], ident_bf16[:]
                )
            nc.scalar.copy(
                out=reduce_bias[:], in_=bias_flipped[:, :, 0:R_PASSES].rearrange("q t g -> q g t")
            )

            span_bias_cols = early.tile([P, P], BF16)
            span_bias_flipped = psum.tile([P, P], BF16, tag="scratch", bufs=SCRATCH_BANKS)
            nc.tensor.transpose(span_bias_flipped[:], span_bias_rows[:], ident_bf16[:])
            nc.scalar.copy(out=span_bias_cols[:], in_=span_bias_flipped[:])

            def spread_span_bias(first_row, rows):
                bank = psum.tile([P, BANK_BF16], BF16, tag="scratch", bufs=SCRATCH_BANKS, name="bias_bank")
                for s in range(rows):
                    nc.tensor.matmul(
                        out=bank[:, P * s : P * (s + 1)],
                        lhsT=span_bias_cols[:, first_row + s : first_row + s + 1].to_broadcast([P, P]),
                        rhs=ident_bf16[:],
                        start=True,
                        stop=True,
                    )
                nc.scalar.copy(
                    out=span_bias[:, P * first_row : P * (first_row + rows)], in_=bank[:, : P * rows]
                )

            def shift_image(tap):
                i, j = divmod(tap, K)
                first = FLAT_PAD + (i - PAD) * W + (j - PAD)
                window = psum.tile([P, C_PASSES, PAIRS, P], F32, tag="scratch", bufs=SCRATCH_BANKS)
                for pt in range(PAIR_TILES):
                    nc.tensor.transpose(
                        window[:, pt // PAIRS, pt % PAIRS, :],
                        x_masked[:, j, pt, first : first + PIX],
                        ident_f32[:],
                    )
                copy_out = nc.scalar.copy if tap % 2 == 0 else nc.vector.tensor_copy
                copy_out(
                    out=shifted[:, tap, :].bitcast(F32).rearrange("n (g p u) -> n g p u", g=C_PASSES, u=PAIRS),
                    in_=window[:].rearrange("n g u p -> n g p u"),
                )

            def reduce_product(chunk):
                raw = early.tile([P, TILES_PER_CHUNK, BANK_F32], F32, bufs=2)
                for a in range(TILES_PER_CHUNK):
                    first_r = REDUCE_CHUNK * chunk + BANK_F32 * a
                    unit, unit_col = divmod(first_r, STREAM_WORDS)
                    quarter, plane_col = divmod(first_r, REDUCE_PLANE_COLS)
                    acc = psum.tile([P, BANK_F32], F32, tag="acc", bufs=ACC_BANKS)
                    for g in range(C_PASSES):
                        nc.tensor.matmul_mx(
                            out=acc[:],
                            lhsT=x_codes[:, g, :].bitcast(FP8X4),
                            lhsT_scale=x_scales[:, g, :],
                            rhs=reduce_words[unit][g][:, unit_col : unit_col + BANK_F32].bitcast(FP8X4),
                            rhs_scale=reduce_planes[
                                ROWS_PER_QUADRANT * quarter : P, g, plane_col : plane_col + BANK_F32
                            ],
                            start=(g == 0),
                            stop=(g == C_PASSES - 1),
                        )
                    nc.scalar.copy(
                        out=raw[:, a, :].rearrange("p (t q) -> p t q", t=PACK),
                        in_=acc[:].rearrange("p (q t) -> p t q", t=PACK),
                    )
                return raw

            def flip_red(chunk, raw):
                biased = early.tile([P, TILES_PER_CHUNK, PIX, PACK], BF16, bufs=2)
                for a in range(TILES_PER_CHUNK):
                    flipped = psum.tile([P, PACK, PIX], F32, tag="scratch", bufs=SCRATCH_BANKS)
                    for t in range(PACK):
                        nc.tensor.transpose(
                            flipped[:, t, :], raw[:, a, P * t : P * (t + 1)], ident_f32[:]
                        )
                    nc.vector.tensor_tensor(
                        out=biased[:, a, :, :],
                        in0=flipped[:].rearrange("q t n -> q n t"),
                        in1=reduce_bias[:, TILES_PER_CHUNK * chunk + a, :]
                        .unsqueeze(1)
                        .to_broadcast([P, PIX, PACK]),
                        op=ALU.add,
                    )
                return biased

            def rectify_red(biased):
                red_grouped = early.tile([P, TILES_PER_CHUNK, PIX, PACK], BF16, bufs=2, align_bytes=64)
                nc.vector.tensor_scalar_max(out=red_grouped[:], in0=biased[:], scalar1=0.0)
                return red_grouped

            def quantise_red(chunk, red_grouped):
                passes = slice(TILES_PER_CHUNK * chunk, TILES_PER_CHUNK * (chunk + 1))
                nc.vector.quantize_mx(
                    out=red_codes[:, passes, :].rearrange("q a n -> q (a n)").bitcast(FP8X4),
                    scales=red_scales[:, passes, :].rearrange("q a n -> q (a n)"),
                    in_=red_grouped[:].rearrange("q a n t -> q (a n t)"),
                )

            for tap in range(TAPS):
                shift_image(tap)
            for first_row in range(0, SPAN_BIAS_ROWS, ROWS_PER_BANK):
                spread_span_bias(first_row, min(ROWS_PER_BANK, SPAN_BIAS_ROWS - first_row))
            raw_ahead = reduce_product(0)
            biased_behind = None
            for chunk in range(REDUCE_CHUNKS):
                raw_now = raw_ahead
                if chunk + 1 < REDUCE_CHUNKS:
                    raw_ahead = reduce_product(chunk + 1)
                if chunk > 0:
                    red_behind = rectify_red(biased_behind)
                biased_now = flip_red(chunk, raw_now)
                if chunk > 0:
                    quantise_red(chunk - 1, red_behind)
                biased_behind = biased_now
            red_behind = rectify_red(biased_behind)
            quantise_red(REDUCE_CHUNKS - 1, red_behind)

        late = ctx.enter_context(tc.tile_pool(name="late", bufs=2))
        products = {}

        stage_banks = []
        first_col = 0
        for end_col in STAGE_ENDS:
            stage_banks.append([])
            while first_col < end_col:
                width = max(w for w in MM_WIDTHS if w <= end_col - first_col)
                stage_banks[-1].append((first_col, width))
                first_col += width
        banks = [bank for numbers in stage_banks for bank in numbers]
        stage_parts = []
        group = 0
        for end_col in STAGE_ENDS:
            end_group = end_col // TAPS
            if end_group < GROUPS - GROUPS_PER_TILE:
                end_group -= end_group % PART_GROUPS
            parts = []
            while group < end_group:
                size = PART_GROUPS
                if group >= GROUPS - GROUPS_PER_TILE:
                    size = LAST_TILE_GROUPS if end_group < GROUPS else LAST_STAGE_GROUPS
                part_end = min(end_group, group + size)
                parts.append((group, part_end))
                group = part_end
            stage_parts.append(parts)
        accs = {}
        exponentials = {}
        totals = {}
        group_inverses = {}
        inverses = {}

        def begin_sum():
            return psum.tile([P, PIX], F32, tag="scratch", bufs=SCRATCH_BANKS, name="summed")

        def add_taps(summed, c_tile, taps, warm_bank):
            for tap in taps:
                if warm_bank is not None and tap % WARM_TAPS == 0:
                    nc.tensor.matmul(
                        out=warm_bank[:],
                        lhsT=ident_bf16[:],
                        rhs=shifted[:, 0, 0:BANK_F32],
                        start=True,
                        stop=True,
                    )
                nc.tensor.matmul(
                    out=summed[:],
                    lhsT=products[c_tile][:, tap, :],
                    rhs=ident_f32[:],
                    start=(tap == 0),
                    stop=(tap == TAPS - 1),
                    is_transpose=True,
                )

        def flip_inverses(c_tiles):
            flipped = psum.tile([P, MAX_READY, PIX], F32, tag="scratch", bufs=SCRATCH_BANKS)
            for i, c_tile in enumerate(c_tiles):
                nc.tensor.transpose(flipped[:, i, :], inverses[c_tile][:], ident_f32[:])
            return flipped

        def copy_inverses(n, flipped):
            rows = late.tile([P, MAX_READY, PIX], F32)
            nc.scalar.copy(out=rows[:, :n, :], in_=flipped[:, :n, :])
            return rows

        def scale_sum(summed, inverse):
            result = late.tile([P, PIX], F32, bufs=PRODUCT_BUFS)
            nc.vector.tensor_tensor(out=result[:], in0=summed[:], in1=inverse, op=ALU.mult)
            return result

        def store(queue, c_tile, result):
            queue.dma_start(out=out_rows[P * c_tile : P * (c_tile + 1), :], in_=result[:])

        def span_product(stage):
            for first_col, width, pass_start, pass_end in SPAN_STAGES[stage]:
                entry_banks = [b for b in banks if first_col <= b[0] < first_col + width]
                if pass_start == 0:
                    for b in entry_banks:
                        accs[b] = psum.tile([P, BANK_F32], F32, tag="acc", bufs=ACC_BANKS, name="acc")
                step = min(MAX_PASSES_PER_LOAD, STREAM_WORDS // width)
                load_ends = list(range(pass_start + step, pass_end, step)) + [pass_end]
                if stage == STAGES - 1:
                    load_ends[-1:] = [pass_end - LAST_PASSES, pass_end]
                first_pass = pass_start
                for end_pass in load_ends:
                    passes = end_pass - first_pass
                    words = stream.tile(
                        [P, STREAM_WORDS], U32, tag="words", name="span_words", align_bytes=64
                    )
                    nc.sync.dma_start(
                        out=words[:, : passes * width].rearrange("p (g n) -> p g n", n=width).bitcast(I32),
                        in_=span_bytes[
                            :, first_pass:end_pass, PACK * first_col : PACK * (first_col + width)
                        ].bitcast(I32),
                    )
                    for g in range(first_pass, end_pass):
                        for bank_col, bank_width in entry_banks:
                            first_word = width * (g - first_pass) + bank_col - first_col
                            nc.tensor.matmul_mx(
                                out=accs[bank_col, bank_width][:, :bank_width],
                                lhsT=red_codes[:, g, :].bitcast(FP8X4),
                                lhsT_scale=red_scales[:, g, :],
                                rhs=words[:, first_word : first_word + bank_width].bitcast(FP8X4),
                                rhs_scale=span_planes[
                                    ROWS_PER_QUADRANT * (g % PLANES_PER_TILE) : P,
                                    g // PLANES_PER_TILE,
                                    bank_col : bank_col + bank_width,
                                ],
                                start=(g == 0),
                                stop=(g == R_PASSES - 1),
                            )
                    first_pass = end_pass

        def add_bias(b):
            first_col, width = b
            cols = slice(first_col, first_col + width)
            nc.vector.tensor_tensor(
                out=kern[:, cols], in0=accs[b][:, :width], in1=span_bias[:, cols], op=ALU.add
            )

        def exponentiate(part):
            first, end = part
            logits = kern[:, TAPS * first : TAPS * end].rearrange("p (g t) -> p g t", t=TAPS)
            minus_top = late.tile([P, PART_GROUPS], F32, bufs=PART_BUFS)
            nc.vector.tensor_reduce(
                out=minus_top[:, : end - first], in_=logits, axis=AXIS_X, op=ALU.max, negate=True
            )
            expd = late.tile([P, PART_GROUPS, TAPS], F32, bufs=PART_BUFS)
            total = late.tile([P, PART_GROUPS], F32, bufs=PART_BUFS)
            for g in range(end - first):
                nc.scalar.activation(
                    out=expd[:, g, :],
                    in_=logits[:, g, :],
                    func=ACT.Exp,
                    bias=minus_top[:, g : g + 1],
                    accum_out=total[:, g : g + 1],
                )
            exponentials[part] = expd
            totals[part] = total

        def invert(part):
            first, end = part
            n = end - first
            c_tile = first // GROUPS_PER_TILE
            if first == GROUPS_PER_TILE * c_tile:
                inverses[c_tile] = late.tile([P, P], F32, name="inverses", bufs=PRODUCT_BUFS)
            group_inverse = late.tile([P, PART_GROUPS], F32, bufs=PART_BUFS)
            nc.vector.reciprocal(out=group_inverse[:, :n], in_=totals[part][:, :n])
            group_inverses[part] = group_inverse

        def spread_inverse(part):
            first, end = part
            n = end - first
            c_tile = first // GROUPS_PER_TILE
            nc.scalar.copy(
                out=inverses[c_tile][
                    :, CH_PER_GROUP * first - P * c_tile : CH_PER_GROUP * end - P * c_tile
                ].rearrange("p (g c) -> p g c", c=CH_PER_GROUP),
                in_=group_inverses[part][:, :n].unsqueeze(2).to_broadcast([P, n, CH_PER_GROUP]),
            )

        def multiply(part, cuts=(0, TAPS)):
            first, end = part
            n = end - first
            c_tile = first // GROUPS_PER_TILE
            if first == GROUPS_PER_TILE * c_tile:
                products[c_tile] = late.tile([P, TAPS, P], F32, name="products", bufs=PRODUCT_BUFS)
            piece = products[c_tile][:, :, CH_PER_GROUP * first - P * c_tile : CH_PER_GROUP * end - P * c_tile]
            images = shifted[:, :, CH_PER_GROUP * first : CH_PER_GROUP * end]
            by_tap = exponentials[part][:, :n, :].rearrange("p g t -> p t g")
            for lo, hi in zip(cuts, cuts[1:]):
                nc.vector.tensor_tensor(
                    out=piece[:, lo:hi, :].rearrange("p t (g c) -> p t g c", c=CH_PER_GROUP),
                    in0=images[:, lo:hi, :].rearrange("p t (g c) -> p t g c", c=CH_PER_GROUP),
                    in1=by_tap[:, lo:hi, :].unsqueeze(3).to_broadcast([P, hi - lo, n, CH_PER_GROUP]),
                    op=ALU.mult,
                )
            return [c_tile] if end == GROUPS_PER_TILE * (c_tile + 1) else []

        ready = []
        waiting = None
        for stage in range(STAGES):
            is_last = stage == STAGES - 1
            span_product(stage)
            to_sum = ready
            ready = []
            warm_bank = None
            if stage >= STAGES - 2:
                warm_bank = psum.tile([P, BANK_F32], F32, tag="acc", bufs=ACC_BANKS)
            flipped = flip_inverses(to_sum) if to_sum else None
            sums = []
            for c_tile in to_sum:
                sums.append(begin_sum())
                add_taps(sums[-1], c_tile, range(TAPS), warm_bank)
            for b in stage_banks[stage]:
                add_bias(b)
            parts = stage_parts[stage]
            for part in parts:
                exponentiate(part)
            inverse_rows = copy_inverses(len(to_sum), flipped) if to_sum else None
            if waiting:
                ready += multiply(waiting)
            waiting = None
            for part in parts:
                invert(part)
                spread_inverse(part)
                if part != parts[-1] or stage == 0:
                    ready += multiply(part)
                elif is_last:
                    ready += multiply(part, (0, TAPS // 2, TAPS))
                else:
                    waiting = part
            for i, c_tile in enumerate(to_sum):
                store(nc.scalar, c_tile, scale_sum(sums[i], inverse_rows[:, i, :]))
        c_tile = ready[-1]
        summed = begin_sum()
        add_taps(summed, c_tile, range(TAPS // 2), warm_bank)
        inverse_rows = copy_inverses(1, flip_inverses([c_tile]))
        add_taps(summed, c_tile, range(TAPS // 2, TAPS), None)
        store(nc.sync, c_tile, scale_sum(summed, inverse_rows[:, 0, :]))
